import numpy as np
import ml_dtypes


def mxq(x, axis, fmt="e4m3"):
    dtype, down = {"e4m3": (ml_dtypes.float8_e4m3fn, 7), "e5m2": (ml_dtypes.float8_e5m2, 14)}[fmt]
    v = np.moveaxis(np.asarray(x, np.float32).astype(ml_dtypes.bfloat16).astype(np.float64), axis, -1)
    blocks = v.reshape(v.shape[:-1] + (-1, 32))
    amax = np.abs(blocks).max(-1, keepdims=True)
    byte = np.maximum(np.where(amax > 0, np.frexp(amax)[1] - 1 + 127, 0) - down, 1)
    scale = np.exp2(byte - 127.0)
    codes = (blocks / scale).astype(np.float32).astype(dtype).astype(np.float64)
    return np.moveaxis((codes * scale).reshape(v.shape), -1, axis)


WIDE = False


def mx_kscale(k):
    if not WIDE:
        return np.ones(k)
    levels = np.array([18, -18])
    if k % 512:
        return np.exp2(np.random.permutation(np.resize(levels, k // 32))).repeat(32)
    a = np.empty((k // 512, 16))
    for p in range(k // 512):
        a[p, :8] = np.random.permutation(np.resize(levels, 8))
        for g in range(8):
            far = levels[np.abs(levels - a[p, g]) >= 10]
            a[p, g + 8] = far[np.random.randint(len(far))]
    return np.exp2(a.ravel()).repeat(32)


BF16 = ml_dtypes.bfloat16


def bf(x):
    return np.asarray(x, np.float32).astype(BF16)


def f64(x):
    return np.asarray(x).astype(np.float64)


B, L, S, T, F, H = 4, 512, 16, 128, 1024, 1024


def setup_inputs():
    u = mx_kscale(L)
    v = mx_kscale(H)
    s = mx_kscale(B * T)
    sr = s.reshape(B, T)
    q0 = bf(np.random.standard_normal((B, L, H)) * 3.0)
    src = bf(np.random.standard_normal((B, S, F)))
    trg0 = bf(np.random.standard_normal((B, T, F)))
    Ws = bf(np.random.standard_normal((F, H)) / np.sqrt(F))
    b_s = bf(np.random.standard_normal(H) * 0.3)
    Wt0 = bf(np.random.standard_normal((F, H)) / np.sqrt(F))
    b_t = bf(np.random.standard_normal(H) * 0.3)
    g = bf(np.random.standard_normal((B, L, T, S)) * np.exp2(np.random.randint(-6, 1, (B, 1, T, 1)))
           * u[None, :, None, None] / sr[:, None, :, None])
    s_key = f64(src) @ f64(Ws) + f64(b_s)
    t_key = f64(trg0) @ f64(Wt0) + f64(b_t)
    return {"q": bf(f64(q0) * v[None, None, :] / u[None, :, None]),
            "src": src,
            "trg": bf(f64(trg0) * sr[:, :, None]),
            "Ws": Ws,
            "b_s": b_s,
            "Wt": bf(f64(Wt0) / v[None, :]),
            "b_t": b_t,
            "s_key": np.asarray(s_key, np.float32),
            "t_key": np.asarray(t_key, np.float32),
            "grad_out": g}


def reference(q, src, trg, Ws, b_s, Wt, b_t, s_key, t_key, grad_out):
    g = f64(grad_out).reshape(B, L, T * S)
    drel = (mxq(g, 1, "e5m2").transpose(0, 2, 1) @ mxq(f64(q), 1, "e4m3")) / np.sqrt(H)
    rel = np.tanh(f64(s_key)[:, None, :, :] + f64(t_key)[:, :, None, :])
    dz1 = (drel.reshape(B, T, S, H) * (1.0 - rel ** 2)).sum(axis=2).reshape(B * T, H)
    dtrg = mxq(dz1, 1, "e5m2") @ mxq(f64(Wt), 1, "e4m3").T
    dWt = mxq(f64(trg).reshape(B * T, F), 0, "e4m3").T @ mxq(dz1, 0, "e5m2")
    return dtrg.reshape(B, T, F), dWt

@@ -1,0 +1,410 @@
+from contextlib import ExitStack
+
+import concourse.mybir as mybir
+from concourse.masks import make_identity
+
+B, L, S, T, F, H = 4, 512, 16, 128, 1024, 1024
+FLOPS = 2 * B * T * S * L * H + 2 * 2 * B * T * F * H
+BYTES = 2 * (B * L * H + B * T * F + F * H + B * L * T * S) + 4 * (B * S * H + B * T * H + B * T * F + F * H)
+
+F32 = mybir.dt.float32
+BF16 = mybir.dt.bfloat16
+U32 = mybir.dt.uint32
+U8 = mybir.dt.uint8
+E4 = mybir.dt.float8_e4m3fn_x4
+E5 = mybir.dt.float8_e5m2_x4
+ALU = mybir.AluOpType
+ACT = mybir.ActivationFunctionType
+
+P = 128
+PACK = 4
+BANK = 512
+TQ = 32
+GROUPS = [(0, 0), (0, 1), (1, 0), (1, 1), (2, 0), (3, 0), (2, 1), (3, 1)]
+UNITS = 4 * len(GROUPS)
+AHEAD = 3
+LOAD_AHEAD = 3
+GP_SQ_STEPS = [21, 22, 23, 24, 25, 27, 28, 29, 30]
+V_SQ_STEPS = list(range(3, 21)) + [26]
+
+
+def tile_dynamicattention4_pa_v_kernel(tc, q, src, trg, Ws, b_s, Wt, b_t, s_key, t_key, grad_out, out_0, out_1):
+    nc = tc.nc
+    with ExitStack() as ctx:
+        sb = ctx.enter_context(tc.tile_pool(name="sb", bufs=1))
+        ps = ctx.enter_context(tc.psum_pool(name="ps", bufs=1))
+        ctx.enter_context(tc.manual_schedule())
+
+        trg_rows = trg.rearrange("b t f -> (b t) f").rearrange("(p j) f -> p j f", j=PACK)
+
+        def source(job):
+            kind, a, c = job
+            cols = slice(c * BANK, (c + 1) * BANK)
+            if kind == "g":
+                return grad_out[a].rearrange("(p j) t s -> p j (t s)", j=PACK)[:, :, cols]
+            if kind == "q":
+                return q[a].rearrange("(p j) h -> p j h", j=PACK)[:, :, cols]
+            return trg_rows[:, :, cols]
+
+        head_jobs = [("q", 0, 0)] + [("g", 0, c) for c in range(4)]
+        step_jobs = [("q", 0, 1)]
+        step_jobs = step_jobs + [("g", 1, c) for c in range(4)] + [("q", 1, 0), ("q", 1, 1)]
+        step_jobs = step_jobs + [("g", 2, c) for c in range(4)] + [("q", 2, 0)]
+        step_jobs = step_jobs + [("g", 3, c) for c in range(4)] + [("q", 3, 0), ("q", 2, 1), ("q", 3, 1)]
+        step_jobs = step_jobs + [("x", 0, 0), ("x", 0, 1)]
+
+        raw, inter, codes = {}, {}, {}
+        code_bufs = {"g": 12, "q": 4, "x": 2}
+
+        def load(job):
+            raw[job] = sb.tile([P, PACK, BANK], BF16, name="raw", bufs=6)
+            nc.sync.dma_start(out=raw[job][:], in_=source(job))
+
+        def interleave_v(dst, rows):
+            nc.vector.tensor_copy(out=dst, in_=rows.rearrange("p j c -> p c j"))
+
+        def interleave_g(dst, rows):
+            nc.gpsimd.tensor_scalar(out=dst, in0=rows.rearrange("p j c -> p c j"), scalar1=1.0, scalar2=1.0,
+                                    op0=ALU.mult, op1=ALU.mult)
+
+        def chain_tile():
+            chain = sb.tile([P, BANK, PACK], BF16, name="chain", bufs=1, align_bytes=64)
+            return chain
+
+        def quantize(job):
+            kind = job[0]
+            words = sb.tile([P, BANK], U32, name="words_" + kind, bufs=code_bufs[kind], align_bytes=64)
+            scales = sb.tile([P, BANK], U8, name="scales_" + kind, bufs=code_bufs[kind], align_bytes=64)
+            nc.vector.quantize_mx(out=words[:].bitcast(E5 if kind == "g" else E4), scales=scales[:],
+                                  in_=inter[job][:].rearrange("p c j -> p (c j)"))
+            codes[job] = (words, scales)
+
+        def mx(out, lhs, lhs_cols, lhs_fmt, rhs, rhs_cols, rhs_fmt, start, stop):
+            nc.tensor.matmul_mx(out=out, lhsT=lhs[0][:, lhs_cols].bitcast(lhs_fmt), lhsT_scale=lhs[1][:, lhs_cols],
+                                rhs=rhs[0][:, rhs_cols].bitcast(rhs_fmt), rhs_scale=rhs[1][:, rhs_cols],
+                                start=start, stop=stop)
+
+        def spare_bank():
+            spare = ps.tile([P, BANK], F32, name="spare", bufs=2)
+            return spare
+
+        def score_bank():
+            score = ps.tile([P, BANK], F32, name="score", bufs=4)
+            return score
+
+        t_rows, t_cols = {}, {}
+
+        def load_t(k):
+            b, half = GROUPS[k]
+            t_rows[k] = sb.tile([P, BANK], F32, name="t_rows", bufs=2)
+            nc.sync.dma_start(out=t_rows[k][:], in_=t_key[b][:, half * BANK:(half + 1) * BANK])
+
+        def transpose4(rows):
+            bank = spare_bank()
+            for c in range(4):
+                nc.tensor.transpose(bank[:, c * P:(c + 1) * P], rows[:, c * P:(c + 1) * P], ident[:])
+            return bank
+
+        def take_t(k, bank):
+            t_cols[k] = sb.tile([P, BANK], F32, name="t_cols", bufs=3)
+            nc.vector.tensor_copy(out=t_cols[k][:], in_=bank[:])
+
+        rel, score, prod, dz_sum, dz_rows = {}, {}, {}, {}, {}
+
+        def tanh(u, s_lo, s_hi):
+            b, half = GROUPS[u // 4]
+            c = u % 4
+            if s_lo == 0:
+                rel[u] = sb.tile([P, 4, S, TQ], F32, name="rel", bufs=AHEAD + 1)
+            for s in range(s_lo, s_hi):
+                col = c * P + 2 * (b * S + s) + half
+                nc.scalar.activation(out=rel[u][:, :, s, :],
+                                     in_=t_cols[u // 4][:, c * P:(c + 1) * P].rearrange("p (a t) -> p a t", a=4),
+                                     func=ACT.Tanh, bias=s_cols[:, col:col + 1])
+
+        def quarters(u, lo, hi):
+            return rel[u][:, lo:hi, :, :].rearrange("p a s t -> p (a s t)")
+
+        def scalar_quarters(u):
+            if u - 1 in GP_SQ_STEPS:
+                return 2
+            if u - 1 in V_SQ_STEPS:
+                return 3
+            return 4
+
+        def square_s(u):
+            part = quarters(u, 0, scalar_quarters(u))
+            nc.scalar.activation(out=part, in_=part, func=ACT.Square, bias=zero[:])
+
+        def square_other(eng, u):
+            part = quarters(u, scalar_quarters(u), 4)
+            eng.tensor_tensor(out=part, in0=part, in1=part, op=ALU.mult)
+
+        def score_mx(u, a):
+            b, half = GROUPS[u // 4]
+            c = u % 4
+            score[u, a] = score_bank()
+            mx(score[u, a][:], codes["q", b, half], slice(c * P, (c + 1) * P), E4,
+               codes["g", b, a], slice(0, BANK), E5, True, True)
+
+        def weigh(u, a):
+            if a == 0:
+                prod[u] = sb.tile([P, S, T], F32, name="prod", bufs=3)
+            nc.vector.scalar_tensor_tensor(out=prod[u][:, :, a * TQ:(a + 1) * TQ], in0=rel[u][:, a, :, :], scalar=1.0,
+                                           in1=score[u, a][:].rearrange("p (t s) -> p s t", s=S),
+                                           op0=ALU.subtract, op1=ALU.mult)
+
+        def sum_s(u, lo, hi):
+            if lo == 0:
+                dz_sum[u] = ps.tile([P, P], F32, name="dz_sum", bufs=2)
+            for s in range(lo, hi):
+                nc.tensor.matmul(out=dz_sum[u][:], lhsT=prod[u][:, s, :], rhs=ident[:], is_transpose=True,
+                                 start=(s == 0), stop=(s == S - 1))
+
+        def round_dz(u):
+            k, c = divmod(u, 4)
+            if c == 0:
+                dz_rows[k] = sb.tile([P, BANK], BF16, name="dz_rows", bufs=3)
+            nc.vector.tensor_scalar(out=dz_rows[k][:, c * P:(c + 1) * P], in0=dz_sum[u][:], scalar1=-1.0 / 32.0,
+                                    scalar2=None, op0=ALU.mult)
+
+        def regroup(k, lo, hi):
+            b, half = GROUPS[k]
+            for j in range(PACK):
+                nc.sync.dma_start(out=z_rows[half][32 * b:32 * (b + 1), j, lo:hi], in_=dz_rows[k][j::PACK, lo:hi])
+
+        w_rows = {}
+
+        def load_w(i):
+            w_rows[i] = sb.tile([P, H], BF16, name="w_rows", bufs=3)
+            nc.sync.dma_start(out=w_rows[i][:], in_=Wt[i * P:(i + 1) * P, :])
+
+        def transpose_w(i):
+            bank = spare_bank()
+            words = w_rows[i][:].bitcast(F32)
+            for g in range(2):
+                for e in range(2):
+                    n = 2 * g + e
+                    nc.tensor.transpose(bank[:, n * P:(n + 1) * P], words[:, 256 * g + e:256 * (g + 1):2], ident[:])
+            return bank
+
+        def take_w(i, bank):
+            nc.vector.tensor_copy(out=w_pairs[:].rearrange("p (g f e) -> p g f e", g=2, e=2)[:, :, i * P:(i + 1) * P, :],
+                                  in_=bank[:].rearrange("p (g e f) -> p g f e", g=2, e=2))
+
+        def quantize_w(n):
+            cols = slice(n * BANK, (n + 1) * BANK)
+            nc.vector.quantize_mx(out=w_codes[0][:, cols].bitcast(E4), scales=w_codes[1][:, cols],
+                                  in_=w_pairs[:, n * 2 * BANK:(n + 1) * 2 * BANK].bitcast(BF16))
+
+        y_pairs, y_codes = {}, {}
+
+        def transpose_y(k):
+            bank = spare_bank()
+            words = dz_rows[k][:].bitcast(F32)
+            for e in range(2):
+                nc.tensor.transpose(bank[:, e * P:(e + 1) * P], words[:, e:2 * P:2], ident[:])
+            return bank
+
+        def take_y(k, bank):
+            y_pairs[k] = sb.tile([P, 2 * P], F32, name="y_pairs", bufs=2, align_bytes=64)
+            nc.vector.tensor_copy(out=y_pairs[k][:].rearrange("p (t e) -> p t e", e=2),
+                                  in_=bank[:, 0:2 * P].rearrange("p (e t) -> p t e", e=2))
+
+        def quantize_y(k):
+            words = sb.tile([P, P], U32, name="y_words", bufs=8, align_bytes=64)
+            scales = sb.tile([P, P], U8, name="y_scales", bufs=8, align_bytes=64)
+            nc.vector.quantize_mx(out=words[:].bitcast(E5), scales=scales[:], in_=y_pairs[k][:].bitcast(BF16))
+            y_codes[GROUPS[k]] = (words, scales)
+
+        def out0_mx(b, n, bank):
+            for g in range(2):
+                mx(bank[:], y_codes[b, g], slice(0, P), E5, w_codes, slice(g * F + n * BANK, g * F + (n + 1) * BANK), E4,
+                   g == 0, g == 1)
+            return bank
+
+        def out1_mx(i, end, bank):
+            c = i % 4
+            mx(bank[:], codes["x", 0, i // 4], slice(c * P, (c + 1) * P), E4, z_codes, slice(end - BANK, end), E5,
+               True, True)
+            return bank
+
+        def store(copy, dst, part):
+            width = part.shape[1]
+            result = sb.tile([P, BANK], F32, name="result", bufs=6)
+            copy(out=result[:, 0:width], in_=part)
+            nc.sync.dma_start(out=dst, in_=result[:, 0:width])
+
+        def store0(copy, b, n, bank):
+            store(copy, out_0[b][:, n * BANK:(n + 1) * BANK], bank[:])
+
+        def store1(copy, i, lo, end, bank):
+            store(copy, out_1[i * P:(i + 1) * P, lo:end], bank[:, BANK - (end - lo):BANK])
+
+        def quantize_z(tile, lo, hi):
+            nc.vector.quantize_mx(out=z_codes[0][:, lo:hi].bitcast(E5), scales=z_codes[1][:, lo:hi],
+                                  in_=tile[:, 0:hi - lo, :].rearrange("p c j -> p (c j)"))
+
+        load_t(0)
+        s_rows = sb.tile([P, BANK], F32, name="s_rows")
+        nc.sync.dma_start(out=s_rows[:], in_=s_key.rearrange("b s (u h) -> (b s u) h", u=2))
+        for job in head_jobs:
+            load(job)
+        load_t(1)
+        load(step_jobs[0])
+
+        ident = sb.tile([P, P], F32, name="ident")
+        make_identity(nc, ident[:])
+        seed = sb.tile([P, 1], F32, name="seed")
+        nc.vector.memset(seed[:], 0.0)
+        zero = sb.tile([P, 1], F32, name="zero")
+        nc.scalar.activation(out=zero[:], in_=seed[:], func=ACT.Tanh, bias=seed[:])
+
+        w_pairs = sb.tile([P, 2 * 2 * F], F32, name="w_pairs", align_bytes=64)
+        w_words = sb.tile([P, 2 * F], U32, name="w_words", align_bytes=64)
+        w_scales = sb.tile([P, 2 * F], U8, name="w_scales", align_bytes=64)
+        w_codes = (w_words, w_scales)
+        z_words = sb.tile([P, H], U32, name="z_words", align_bytes=64)
+        z_scales = sb.tile([P, H], U8, name="z_scales", align_bytes=64)
+        z_codes = (z_words, z_scales)
+        z_rows0 = sb.tile([P, PACK, BANK], BF16, name="z_rows0")
+        z_rows1 = sb.tile([P, PACK, BANK], BF16, name="z_rows1")
+        z_rows = (z_rows0, z_rows1)
+
+        t_bank = transpose4(t_rows[0])
+        s_bank = transpose4(s_rows)
+        take_t(0, t_bank)
+        s_cols = sb.tile([P, BANK], F32, name="s_cols")
+        nc.vector.tensor_copy(out=s_cols[:], in_=s_bank[:])
+        t_bank = transpose4(t_rows[1])
+
+        for n, job in enumerate(head_jobs):
+            if n == len(head_jobs) - 1:
+                inter[job] = chain_tile()
+            else:
+                inter[job] = sb.tile([P, BANK, PACK], BF16, name="head", bufs=2, align_bytes=64)
+            interleave_v(inter[job][:], raw[job][:])
+            if n > 0:
+                quantize(head_jobs[n - 1])
+        take_t(1, t_bank)
+        quantize(head_jobs[-1])
+        for n in range(1, LOAD_AHEAD):
+            load(step_jobs[n])
+        load_w(0)
+        load_w(1)
+        for a in range(4):
+            score_mx(0, a)
+        tanh(0, 0, S)
+        for u in range(1, AHEAD):
+            tanh(u, 0, 2)
+            square_s(u - 1)
+            tanh(u, 2, S)
+
+        w_steps = [0, 1, 2, 4, 5, 6, 8, 9]
+        out0_steps = {14: (0, 0), 16: (0, 1), 20: (1, 0), 22: (1, 1)}
+        out1_steps = {27: [0, 1], 28: [2, 3], 29: [4], 30: [5, 6]}
+        filled = []
+        for step in range(UNITS):
+            last = step == UNITS - 1
+            if step + LOAD_AHEAD < len(step_jobs):
+                load(step_jobs[step + LOAD_AHEAD])
+            if step + 2 in w_steps:
+                load_w(w_steps.index(step + 2))
+            if step % 4 == 1 and step // 4 + 2 < len(GROUPS):
+                load_t(step // 4 + 2)
+            job = step_jobs[step] if step < len(step_jobs) else None
+            if job is not None:
+                inter[job] = chain_tile()
+                interleave_g(inter[job][:], raw[job][:])
+            if step == 26:
+                z_tile = chain_tile()
+                interleave_g(z_tile[:], z_rows[0][:])
+            if last:
+                z_tile = chain_tile()
+                interleave_g(z_tile[:, 0:256, :], z_rows[1][:, :, 0:256])
+            if step in GP_SQ_STEPS:
+                square_other(nc.gpsimd, step + 1)
+            if step + AHEAD < UNITS:
+                tanh(step + AHEAD, 0, 2)
+            if step + AHEAD - 1 < UNITS:
+                square_s(step + AHEAD - 1)
+            if step + AHEAD < UNITS:
+                tanh(step + AHEAD, 2, S)
+            for a in (0, 1):
+                weigh(step, a)
+                if not last:
+                    score_mx(step + 1, a)
+            if step > 0:
+                sum_s(step - 1, S // 2, S)
+            quantize_late = []
+            for kind, arg, bank in filled:
+                if kind == "t":
+                    take_t(arg, bank)
+                if kind == "w":
+                    take_w(arg, bank)
+                if kind == "y":
+                    take_y(arg, bank)
+                    quantize_late.append(arg)
+                if kind == "o0":
+                    store0(nc.vector.tensor_copy, arg[0], arg[1], bank)
+                if kind == "o1":
+                    store1(nc.scalar.copy if last else nc.vector.tensor_copy, arg, 0, BANK, bank)
+            filled = []
+            if last:
+                store1(nc.scalar.copy, 7, 0, BANK, out1_mx(7, BANK, spare_bank()))
+                store0(nc.scalar.copy, 2, 0, out0_mx(2, 0, spare_bank()))
+                store0(nc.scalar.copy, 2, 1, out0_mx(2, 1, score_bank()))
+            for a in (2, 3):
+                weigh(step, a)
+                if not last:
+                    score_mx(step + 1, a)
+            if step > 0:
+                round_dz(step - 1)
+                if step % 4 == 0:
+                    regroup(step // 4 - 1, 0, BANK)
+                if step == UNITS - 2:
+                    regroup(7, 0, 256)
+                if last:
+                    regroup(7, 256, 384)
+            sum_s(step, 0, S if last else S // 2)
+            if step in V_SQ_STEPS:
+                square_other(nc.vector, step + 1)
+            for k in quantize_late:
+                quantize_y(k)
+            if 10 <= step < 14:
+                quantize_w(step - 10)
+            if job is not None:
+                quantize(job)
+            if step == 26:
+                quantize_z(z_tile, 0, BANK)
+            if last:
+                quantize_z(z_tile, BANK, BANK + 256)
+            if step % 4 == 3 and step // 4 + 2 < len(GROUPS):
+                filled.append(("t", step // 4 + 2, transpose4(t_rows[step // 4 + 2])))
+            if step in w_steps:
+                filled.append(("w", w_steps.index(step), transpose_w(w_steps.index(step))))
+            if step % 4 == 1 and step > 4:
+                filled.append(("y", step // 4 - 1, transpose_y(step // 4 - 1)))
+            if step in out0_steps:
+                b, n = out0_steps[step]
+                filled.append(("o0", (b, n), out0_mx(b, n, spare_bank())))
+            for i in out1_steps.get(step, []):
+                filled.append(("o1", i, out1_mx(i, BANK, spare_bank())))
+
+        round_dz(UNITS - 1)
+        regroup(7, 384, BANK)
+        y_bank = transpose_y(7)
+        take_y(7, y_bank)
+        copies = (nc.scalar.copy, nc.vector.tensor_copy)
+        for i in range(4):
+            store1(nc.scalar.copy, i, BANK, BANK + 256, out1_mx(i, BANK + 256, score_bank()))
+        quantize_y(7)
+        for i in range(4, 8):
+            store1(copies[i % 2], i, BANK, BANK + 256, out1_mx(i, BANK + 256, score_bank()))
+        z_tile = chain_tile()
+        interleave_v(z_tile[:, 0:256, :], z_rows[1][:, :, 256:BANK])
+        for n in range(2):
+            store0(nc.scalar.copy, 3, n, out0_mx(3, n, spare_bank()))
+        quantize_z(z_tile, BANK + 256, H)
+        for i in range(8):
+            store1(copies[i % 2], i, BANK + 256, H, out1_mx(i, H, score_bank()))

@@ -20,12 +20,21 @@ P = 128
 PACK = 4
 BANK = 512
 TQ = 32
-GROUPS = [(0, 0), (0, 1), (1, 0), (1, 1), (2, 0), (3, 0), (2, 1), (3, 1)]
+GROUPS = [(b, half) for b in range(B) for half in range(2)]
 UNITS = 4 * len(GROUPS)
 AHEAD = 3
 LOAD_AHEAD = 3
-GP_SQ_STEPS = [21, 22, 23, 24, 25, 27, 28, 29, 30]
-V_SQ_STEPS = list(range(3, 21)) + [26]
+HALF = BANK // 2
+UNIT_COLS = S * T
+GP_SQ_SINGLE = 256
+GP_SQ_LATE = 384
+V_SQ_SINGLE = 512
+V_SQ_DOUBLE = 384
+V_SQ_LATE = 384
+SPLIT = 8
+V_SQ_FROM = 1
+V_SQ_TO = 31
+WARM = (0, 8)
 
 
 def tile_dynamicattention4_pa_v_kernel(tc, q, src, trg, Ws, b_s, Wt, b_t, s_key, t_key, grad_out, out_0, out_1):
@@ -47,14 +56,17 @@ def tile_dynamicattention4_pa_v_kernel(tc, q, src, trg, Ws, b_s, Wt, b_t, s_key,
             return trg_rows[:, :, cols]
 
         head_jobs = [("q", 0, 0)] + [("g", 0, c) for c in range(4)]
-        step_jobs = [("q", 0, 1)]
-        step_jobs = step_jobs + [("g", 1, c) for c in range(4)] + [("q", 1, 0), ("q", 1, 1)]
-        step_jobs = step_jobs + [("g", 2, c) for c in range(4)] + [("q", 2, 0)]
-        step_jobs = step_jobs + [("g", 3, c) for c in range(4)] + [("q", 3, 0), ("q", 2, 1), ("q", 3, 1)]
-        step_jobs = step_jobs + [("x", 0, 0), ("x", 0, 1)]
+        jobs = []
+        for b in range(1, B):
+            jobs = jobs + [("q", b - 1, 1)] + [("g", b, c) for c in range(4)] + [("q", b, 0)]
+        jobs = jobs + [("q", B - 1, 1), ("x", 0, 0), ("x", 0, 1)]
+        pieces = [(job, h) for job in jobs for h in range(2)]
+        counts = [2, 2, 2, 1, 2, 2, 1] + [2, 1] * 8 + [1, 2, 1, 1, 1] + [0] * 4
+        starts = [sum(counts[:n]) for n in range(UNITS + 1)]
+        step_pieces = [pieces[starts[n]:starts[n + 1]] for n in range(UNITS)]
 
         raw, inter, codes = {}, {}, {}
-        code_bufs = {"g": 12, "q": 4, "x": 2}
+        code_bufs = {"g": 8, "q": 4, "x": 2}
 
         def load(job):
             raw[job] = sb.tile([P, PACK, BANK], BF16, name="raw", bufs=6)
@@ -67,17 +79,19 @@ def tile_dynamicattention4_pa_v_kernel(tc, q, src, trg, Ws, b_s, Wt, b_t, s_key,
             nc.gpsimd.tensor_scalar(out=dst, in0=rows.rearrange("p j c -> p c j"), scalar1=1.0, scalar2=1.0,
                                     op0=ALU.mult, op1=ALU.mult)
 
-        def chain_tile():
-            chain = sb.tile([P, BANK, PACK], BF16, name="chain", bufs=1, align_bytes=64)
+        def chain_tile(h):
+            chain = sb.tile([P, HALF, PACK], BF16, name="chain%d" % h, bufs=1, align_bytes=64)
             return chain
 
-        def quantize(job):
+        def quantize(job, h, tile):
             kind = job[0]
-            words = sb.tile([P, BANK], U32, name="words_" + kind, bufs=code_bufs[kind], align_bytes=64)
-            scales = sb.tile([P, BANK], U8, name="scales_" + kind, bufs=code_bufs[kind], align_bytes=64)
-            nc.vector.quantize_mx(out=words[:].bitcast(E5 if kind == "g" else E4), scales=scales[:],
-                                  in_=inter[job][:].rearrange("p c j -> p (c j)"))
-            codes[job] = (words, scales)
+            if h == 0:
+                words = sb.tile([P, BANK], U32, name="words_" + kind, bufs=code_bufs[kind], align_bytes=64)
+                scales = sb.tile([P, BANK], U8, name="scales_" + kind, bufs=code_bufs[kind], align_bytes=64)
+                codes[job] = (words, scales)
+            cols = slice(h * HALF, h * HALF + tile.shape[1])
+            nc.vector.quantize_mx(out=codes[job][0][:, cols].bitcast(E5 if kind == "g" else E4),
+                                  scales=codes[job][1][:, cols], in_=tile.rearrange("p c j -> p (c j)"))
 
         def mx(out, lhs, lhs_cols, lhs_fmt, rhs, rhs_cols, rhs_fmt, start, stop):
             nc.tensor.matmul_mx(out=out, lhsT=lhs[0][:, lhs_cols].bitcast(lhs_fmt), lhsT_scale=lhs[1][:, lhs_cols],
@@ -122,23 +136,33 @@ def tile_dynamicattention4_pa_v_kernel(tc, q, src, trg, Ws, b_s, Wt, b_t, s_key,
                                      in_=t_cols[u // 4][:, c * P:(c + 1) * P].rearrange("p (a t) -> p a t", a=4),
                                      func=ACT.Tanh, bias=s_cols[:, col:col + 1])
 
-        def quarters(u, lo, hi):
-            return rel[u][:, lo:hi, :, :].rearrange("p a s t -> p (a s t)")
+        def columns(u, lo, hi):
+            return rel[u][:].rearrange("p a s t -> p (a s t)")[:, lo:hi]
 
-        def scalar_quarters(u):
-            if u - 1 in GP_SQ_STEPS:
-                return 2
-            if u - 1 in V_SQ_STEPS:
-                return 3
-            return 4
+        def shares(u):
+            step = u - 1
+            if step < 0:
+                return UNIT_COLS, UNIT_COLS
+            n = counts[step]
+            gp = 0 if n == 2 or step >= 30 else (GP_SQ_SINGLE if step < 23 else GP_SQ_LATE)
+            ve = (V_SQ_DOUBLE if n == 2 else (V_SQ_SINGLE if step < 23 else V_SQ_LATE)) if V_SQ_FROM <= step < V_SQ_TO else 0
+            return UNIT_COLS - gp - ve, UNIT_COLS - gp
 
         def square_s(u):
-            part = quarters(u, 0, scalar_quarters(u))
+            part = columns(u, 0, shares(u)[0])
             nc.scalar.activation(out=part, in_=part, func=ACT.Square, bias=zero[:])
 
-        def square_other(eng, u):
-            part = quarters(u, scalar_quarters(u), 4)
-            eng.tensor_tensor(out=part, in0=part, in1=part, op=ALU.mult)
+        def square_v(u):
+            lo, hi = shares(u)
+            if hi > lo:
+                part = columns(u, lo, hi)
+                nc.vector.tensor_tensor(out=part, in0=part, in1=part, op=ALU.mult)
+
+        def square_g(u):
+            lo = shares(u)[1]
+            if lo < UNIT_COLS:
+                part = columns(u, lo, UNIT_COLS)
+                nc.gpsimd.tensor_tensor(out=part, in0=part, in1=part, op=ALU.mult)
 
         def score_mx(u, a):
             b, half = GROUPS[u // 4]
@@ -158,7 +182,7 @@ def tile_dynamicattention4_pa_v_kernel(tc, q, src, trg, Ws, b_s, Wt, b_t, s_key,
             if lo == 0:
                 dz_sum[u] = ps.tile([P, P], F32, name="dz_sum", bufs=2)
             for s in range(lo, hi):
-                nc.tensor.matmul(out=dz_sum[u][:], lhsT=prod[u][:, s, :], rhs=ident[:], is_transpose=True,
+                nc.tensor.matmul(out=dz_sum[u][:], lhsT=prod[u][:, s, :], rhs=ident[:], is_transpose=(s not in WARM or u >= 29),
                                  start=(s == 0), stop=(s == S - 1))
 
         def round_dz(u):
@@ -173,10 +197,29 @@ def tile_dynamicattention4_pa_v_kernel(tc, q, src, trg, Ws, b_s, Wt, b_t, s_key,
             for j in range(PACK):
                 nc.sync.dma_start(out=z_rows[half][32 * b:32 * (b + 1), j, lo:hi], in_=dz_rows[k][j::PACK, lo:hi])
 
+        def finish(u):
+            round_dz(u)
+            if u < 24 and u % 4 == 3:
+                regroup(u // 4, 0, BANK)
+            if u >= 24 and u % 4 == 1:
+                regroup(u // 4, 0, HALF)
+            if u >= 24 and u % 4 == 2:
+                regroup(u // 4, HALF, HALF + P)
+
+        def pick_rows(k):
+            bank = spare_bank()
+            for j in range(PACK):
+                nc.tensor.matmul(out=bank[:, j * P:(j + 1) * P], lhsT=pick[:, j, :], rhs=dz_rows[k][:, HALF + P:BANK],
+                                 start=True, stop=True)
+            return bank
+
+        def take_picked(tile, bank):
+            nc.vector.tensor_copy(out=tile[96:P, P:HALF, :], in_=bank[96:P, :].rearrange("p (j c) -> p c j", j=PACK))
+
         w_rows = {}
 
         def load_w(i):
-            w_rows[i] = sb.tile([P, H], BF16, name="w_rows", bufs=3)
+            w_rows[i] = sb.tile([P, H], BF16, name="w_rows", bufs=4)
             nc.sync.dma_start(out=w_rows[i][:], in_=Wt[i * P:(i + 1) * P, :])
 
         def transpose_w(i):
@@ -229,17 +272,28 @@ def tile_dynamicattention4_pa_v_kernel(tc, q, src, trg, Ws, b_s, Wt, b_t, s_key,
                True, True)
             return bank
 
-        def store(copy, dst, part):
-            width = part.shape[1]
-            result = sb.tile([P, BANK], F32, name="result", bufs=6)
-            copy(out=result[:, 0:width], in_=part)
-            nc.sync.dma_start(out=dst, in_=result[:, 0:width])
-
         def store0(copy, b, n, bank):
-            store(copy, out_0[b][:, n * BANK:(n + 1) * BANK], bank[:])
+            result = sb.tile([P, BANK], F32, name="result", bufs=8)
+            copy(out=result[:], in_=bank[:])
+            nc.sync.dma_start(out=out_0[b][:, n * BANK:(n + 1) * BANK], in_=result[:])
 
-        def store1(copy, i, lo, end, bank):
-            store(copy, out_1[i * P:(i + 1) * P, lo:end], bank[:, BANK - (end - lo):BANK])
+        def store0x(copy, i, bank):
+            result = sb.tile([P, BANK], F32, name="result", bufs=8)
+            copy(out=result[:], in_=bank[:])
+            nc.sync.dma_start(out=out_1[i * P:(i + 1) * P, BANK:H], in_=result[:])
+
+        wide = {}
+
+        def store1(copy, i, lo, end, bank, queue=nc.scalar):
+            width = end - lo
+            count = 2 * BANK // width
+            first = i - i % count
+            if i == first:
+                wide[lo] = sb.tile([P, count, width], F32, name="wide", bufs=4)
+            copy(out=wide[lo][:, i - first, :], in_=bank[:, BANK - width:BANK])
+            if i == first + count - 1:
+                rows = out_1[first * P:(first + count) * P, lo:end].rearrange("(n p) c -> p n c", p=P)
+                queue.dma_start(out=rows, in_=wide[lo][:])
 
         def quantize_z(tile, lo, hi):
             nc.vector.quantize_mx(out=z_codes[0][:, lo:hi].bitcast(E5), scales=z_codes[1][:, lo:hi],
@@ -250,8 +304,8 @@ def tile_dynamicattention4_pa_v_kernel(tc, q, src, trg, Ws, b_s, Wt, b_t, s_key,
         nc.sync.dma_start(out=s_rows[:], in_=s_key.rearrange("b s (u h) -> (b s u) h", u=2))
         for job in head_jobs:
             load(job)
+        load(jobs[0])
         load_t(1)
-        load(step_jobs[0])
 
         ident = sb.tile([P, P], F32, name="ident")
         make_identity(nc, ident[:])
@@ -271,59 +325,76 @@ def tile_dynamicattention4_pa_v_kernel(tc, q, src, trg, Ws, b_s, Wt, b_t, s_key,
         z_rows1 = sb.tile([P, PACK, BANK], BF16, name="z_rows1")
         z_rows = (z_rows0, z_rows1)
 
+        pick = sb.tile([P, PACK, P], BF16, name="pick")
+        nc.gpsimd.memset(pick[:], 0.0)
+        nc.gpsimd.tensor_copy(out=pick[:, :, 96:P], in_=ident[:].rearrange("p (i j) -> p j i", j=PACK))
         t_bank = transpose4(t_rows[0])
         s_bank = transpose4(s_rows)
         take_t(0, t_bank)
         s_cols = sb.tile([P, BANK], F32, name="s_cols")
         nc.vector.tensor_copy(out=s_cols[:], in_=s_bank[:])
-        t_bank = transpose4(t_rows[1])
 
-        for n, job in enumerate(head_jobs):
-            if n == len(head_jobs) - 1:
-                inter[job] = chain_tile()
-            else:
-                inter[job] = sb.tile([P, BANK, PACK], BF16, name="head", bufs=2, align_bytes=64)
+        for n, job in enumerate(head_jobs[:-1]):
+            inter[job] = sb.tile([P, BANK, PACK], BF16, name="head", bufs=2, align_bytes=64)
             interleave_v(inter[job][:], raw[job][:])
             if n > 0:
-                quantize(head_jobs[n - 1])
-        take_t(1, t_bank)
-        quantize(head_jobs[-1])
-        for n in range(1, LOAD_AHEAD):
-            load(step_jobs[n])
-        load_w(0)
-        load_w(1)
+                quantize(head_jobs[n - 1], 0, inter[head_jobs[n - 1]][:])
+        job = head_jobs[-1]
+        for h in range(2):
+            inter[job, h] = chain_tile(h)
+            interleave_v(inter[job, h][:], raw[job][:, :, h * HALF:(h + 1) * HALF])
+        quantize(head_jobs[-2], 0, inter[head_jobs[-2]][:])
+        for h in range(2):
+            quantize(job, h, inter[job, h][:])
+        loaded = LOAD_AHEAD
+        for n in range(1, loaded):
+            load(jobs[n])
+        for i in range(4):
+            load_w(i)
         for a in range(4):
             score_mx(0, a)
+        t_bank = transpose4(t_rows[1])
         tanh(0, 0, S)
         for u in range(1, AHEAD):
             tanh(u, 0, 2)
             square_s(u - 1)
             tanh(u, 2, S)
 
-        w_steps = [0, 1, 2, 4, 5, 6, 8, 9]
-        out0_steps = {14: (0, 0), 16: (0, 1), 20: (1, 0), 22: (1, 1)}
-        out1_steps = {27: [0, 1], 28: [2, 3], 29: [4], 30: [5, 6]}
-        filled = []
+        wq_steps = {3: 0, 6: 2, 10: 1, 12: 3}
+        fills = {0: [("w", 0), ("w", 1)], 1: [("w", 2), ("w", 3)], 3: [("t", 2), ("w", 4)], 4: [("w", 5), ("w", 6)],
+                 6: [("t", 3), ("y", 0)], 8: [("w", 7)], 10: [("t", 4), ("y", 1)], 12: [("o0", (0, 0))],
+                 14: [("t", 5), ("y", 2)], 16: [("o0", (0, 1))], 18: [("t", 6), ("y", 3)],
+                 20: [("o0", (1, 0)), ("o0", (1, 1))], 23: [("t", 7), ("y", 4)], 25: [("y", 5)],
+                 26: [("o0", (2, 0))], 27: [("o0", (2, 1))], 29: [("y", 6)]}
+        filled = [("t", 1, t_bank)]
         for step in range(UNITS):
             last = step == UNITS - 1
-            if step + LOAD_AHEAD < len(step_jobs):
-                load(step_jobs[step + LOAD_AHEAD])
-            if step + 2 in w_steps:
-                load_w(w_steps.index(step + 2))
-            if step % 4 == 1 and step // 4 + 2 < len(GROUPS):
-                load_t(step // 4 + 2)
-            job = step_jobs[step] if step < len(step_jobs) else None
-            if job is not None:
-                inter[job] = chain_tile()
-                interleave_g(inter[job][:], raw[job][:])
-            if step == 26:
-                z_tile = chain_tile()
-                interleave_g(z_tile[:], z_rows[0][:])
+            while loaded < len(jobs) and 2 * loaded < starts[min(step + LOAD_AHEAD + 1, UNITS)]:
+                load(jobs[loaded])
+                loaded = loaded + 1
+            for kind, arg in fills.get(step + 2, []):
+                if kind == "w":
+                    load_w(arg)
+                if kind == "t":
+                    load_t(arg)
+            for n, (job, h) in enumerate(step_pieces[step]):
+                inter[job, h] = chain_tile(n)
+                interleave_g(inter[job, h][:], raw[job][:, :, h * HALF:(h + 1) * HALF])
+            z_tiles = []
             if last:
-                z_tile = chain_tile()
-                interleave_g(z_tile[:, 0:256, :], z_rows[1][:, :, 0:256])
-            if step in GP_SQ_STEPS:
-                square_other(nc.gpsimd, step + 1)
+                z_last = chain_tile(1)
+            for lo in {28: (0,), 31: (BANK,)}.get(step, ()):
+                z_tile = chain_tile(0)
+                interleave_g(z_tile[:], z_rows[lo // BANK][:, :, 0:HALF])
+                z_tiles.append((z_tile, lo))
+            if step == 29:
+                z_tile = chain_tile(0)
+                interleave_g(z_tile[0:96, P:HALF, :], z_rows[0][0:96, :, HALF + P:BANK])
+                interleave_g(z_tile[:, 0:P, :], z_rows[0][:, :, HALF:HALF + P])
+                z_tiles.append((z_tile, HALF))
+                filled.append(("pick", z_tile, pick_rows(6)))
+            if not last:
+                square_g(step + 1)
             if step + AHEAD < UNITS:
                 tanh(step + AHEAD, 0, 2)
             if step + AHEAD - 1 < UNITS:
@@ -332,10 +403,21 @@ def tile_dynamicattention4_pa_v_kernel(tc, q, src, trg, Ws, b_s, Wt, b_t, s_key,
                 tanh(step + AHEAD, 2, S)
             for a in (0, 1):
                 weigh(step, a)
-                if not last:
+                if last:
+                    store1(nc.scalar.copy, 4 + a, 0, BANK, out1_mx(4 + a, BANK, score_bank()))
+                else:
                     score_mx(step + 1, a)
             if step > 0:
-                sum_s(step - 1, S // 2, S)
+                sum_s(step - 1, SPLIT, S)
+            if 2 <= step < 28:
+                finish(step - 2)
+            if step == UNITS - 2:
+                for i in (0, 1):
+                    store1(nc.scalar.copy, i, 0, BANK, out1_mx(i, BANK, spare_bank()))
+            for a in (2, 3):
+                weigh(step, a)
+                if not last:
+                    score_mx(step + 1, a)
             quantize_late = []
             for kind, arg, bank in filled:
                 if kind == "t":
@@ -345,66 +427,52 @@ def tile_dynamicattention4_pa_v_kernel(tc, q, src, trg, Ws, b_s, Wt, b_t, s_key,
                 if kind == "y":
                     take_y(arg, bank)
                     quantize_late.append(arg)
+                if kind == "pick":
+                    take_picked(arg, bank)
                 if kind == "o0":
                     store0(nc.vector.tensor_copy, arg[0], arg[1], bank)
-                if kind == "o1":
-                    store1(nc.scalar.copy if last else nc.vector.tensor_copy, arg, 0, BANK, bank)
             filled = []
-            if last:
-                store1(nc.scalar.copy, 7, 0, BANK, out1_mx(7, BANK, spare_bank()))
-                store0(nc.scalar.copy, 2, 0, out0_mx(2, 0, spare_bank()))
-                store0(nc.scalar.copy, 2, 1, out0_mx(2, 1, score_bank()))
-            for a in (2, 3):
-                weigh(step, a)
-                if not last:
-                    score_mx(step + 1, a)
-            if step > 0:
-                round_dz(step - 1)
-                if step % 4 == 0:
-                    regroup(step // 4 - 1, 0, BANK)
-                if step == UNITS - 2:
-                    regroup(7, 0, 256)
-                if last:
-                    regroup(7, 256, 384)
-            sum_s(step, 0, S if last else S // 2)
-            if step in V_SQ_STEPS:
-                square_other(nc.vector, step + 1)
+            sum_s(step, 0, S if last else SPLIT)
+            if step == UNITS - 2:
+                for i in (2, 3):
+                    store1(nc.scalar.copy, i, 0, BANK, out1_mx(i, BANK, spare_bank()))
+            if not last:
+                square_v(step + 1)
             for k in quantize_late:
                 quantize_y(k)
-            if 10 <= step < 14:
-                quantize_w(step - 10)
-            if job is not None:
-                quantize(job)
-            if step == 26:
-                quantize_z(z_tile, 0, BANK)
+            if step in wq_steps:
+                quantize_w(wq_steps[step])
+            for job, h in step_pieces[step]:
+                quantize(job, h, inter[job, h][:])
             if last:
-                quantize_z(z_tile, BANK, BANK + 256)
-            if step % 4 == 3 and step // 4 + 2 < len(GROUPS):
-                filled.append(("t", step // 4 + 2, transpose4(t_rows[step // 4 + 2])))
-            if step in w_steps:
-                filled.append(("w", w_steps.index(step), transpose_w(w_steps.index(step))))
-            if step % 4 == 1 and step > 4:
-                filled.append(("y", step // 4 - 1, transpose_y(step // 4 - 1)))
-            if step in out0_steps:
-                b, n = out0_steps[step]
-                filled.append(("o0", (b, n), out0_mx(b, n, spare_bank())))
-            for i in out1_steps.get(step, []):
-                filled.append(("o1", i, out1_mx(i, BANK, spare_bank())))
+                finish(step - 1)
+                interleave_v(z_last[0:96, P:HALF, :], z_rows[1][0:96, :, HALF + P:BANK])
+                round_dz(step)
+            for z_tile, lo in z_tiles:
+                quantize_z(z_tile, lo, lo + HALF)
+            if 27 <= step < UNITS - 1:
+                finish(step - 1)
+            for kind, arg in fills.get(step, []):
+                if kind == "t":
+                    filled.append((kind, arg, transpose4(t_rows[arg])))
+                if kind == "w":
+                    filled.append((kind, arg, transpose_w(arg)))
+                if kind == "y":
+                    filled.append((kind, arg, transpose_y(arg)))
+                if kind == "o0":
+                    filled.append((kind, arg, out0_mx(arg[0], arg[1], spare_bank())))
 
-        round_dz(UNITS - 1)
-        regroup(7, 384, BANK)
-        y_bank = transpose_y(7)
-        take_y(7, y_bank)
         copies = (nc.scalar.copy, nc.vector.tensor_copy)
-        for i in range(4):
-            store1(nc.scalar.copy, i, BANK, BANK + 256, out1_mx(i, BANK + 256, score_bank()))
+        for i in (6, 7):
+            store1(nc.scalar.copy, i, 0, BANK, out1_mx(i, BANK, score_bank()))
+        picked = pick_rows(7)
+        y_bank = transpose_y(7)
+        take_picked(z_last, picked)
+        take_y(7, y_bank)
+        interleave_v(z_last[:, 0:P, :], z_rows[1][:, :, HALF:HALF + P])
         quantize_y(7)
-        for i in range(4, 8):
-            store1(copies[i % 2], i, BANK, BANK + 256, out1_mx(i, BANK + 256, score_bank()))
-        z_tile = chain_tile()
-        interleave_v(z_tile[:, 0:256, :], z_rows[1][:, :, 256:BANK])
+        quantize_z(z_last, BANK + HALF, H)
         for n in range(2):
-            store0(nc.scalar.copy, 3, n, out0_mx(3, n, spare_bank()))
-        quantize_z(z_tile, BANK + 256, H)
+            store0(nc.scalar.copy, 3, n, out0_mx(3, n, score_bank()))
         for i in range(8):
-            store1(copies[i % 2], i, BANK + 256, H, out1_mx(i, H, score_bank()))
+            store0x(copies[(i + 1) % 2], i, out1_mx(i, H, score_bank() if i % 3 else spare_bank()))

@@ -1,3 +1,4 @@
+import math
 from contextlib import ExitStack
 
 import concourse.mybir as mybir
@@ -11,111 +12,138 @@ F32 = mybir.dt.float32
 BF16 = mybir.dt.bfloat16
 U32 = mybir.dt.uint32
 U8 = mybir.dt.uint8
-E4 = mybir.dt.float8_e4m3fn_x4
-E5 = mybir.dt.float8_e5m2_x4
+E4M3 = mybir.dt.float8_e4m3fn_x4
+E5M2 = mybir.dt.float8_e5m2_x4
 ALU = mybir.AluOpType
 ACT = mybir.ActivationFunctionType
 
 P = 128
 PACK = 4
 BANK = 512
-TQ = 32
-GROUPS = [(b, half) for b in range(B) for half in range(2)]
-UNITS = 4 * len(GROUPS)
+PIECE = BANK // 2
+BANK_TOKENS = BANK // S
+UNIT_BANKS = T // BANK_TOKENS
+GROUP = BANK // P
+GROUPS = B * H // BANK
+UNITS = GROUP * GROUPS
+LAST_ROWS = P - T // PACK
+
 AHEAD = 3
 LOAD_AHEAD = 3
-HALF = BANK // 2
-UNIT_COLS = S * T
-GP_SQ_SINGLE = 256
-GP_SQ_LATE = 384
-V_SQ_SINGLE = 512
-V_SQ_DOUBLE = 384
-V_SQ_LATE = 384
-SPLIT = 8
-V_SQ_FROM = 1
-V_SQ_TO = 31
-WARM = (0, 8)
+PLAIN_S = (0, 8)
+CLOSING = UNITS - 5
+
+GPSIMD_SQUARES = 256
+GPSIMD_SQUARES_LAST_B = 384
+VECTOR_SQUARES_ONE_PIECE = 512
+VECTOR_SQUARES = 384
 
 
-def tile_dynamicattention4_pa_v_kernel(tc, q, src, trg, Ws, b_s, Wt, b_t, s_key, t_key, grad_out, out_0, out_1):
+def spread(total, steps):
+    done = [math.ceil(total * n / steps) for n in range(steps + 1)]
+    return [done[n + 1] - done[n] for n in range(steps)]
+
+
+def plan_fills(piece_counts, last_b_from):
+    waiting = [(GROUP * k - 6, "t", k) for k in range(2, GROUPS)]
+    waiting = waiting + [(GROUP * k + 5, "dz", k) for k in range(GROUPS - 1)]
+    waiting = waiting + [(0, "w", i) for i in range(F // P)]
+    waiting = waiting + [(12 + n, "out_0", (0, n)) for n in range(2)]
+    waiting = waiting + [(2 * GROUP * b + 10, "out_0", (b, n)) for b in range(1, B - 1) for n in range(2)]
+    fills = []
+    for step in range(UNITS - 1):
+        room = 2 if piece_counts[step + 1] == 2 else (1 if step >= last_b_from else 0)
+        taken = [item for item in waiting if item[0] <= step][:room]
+        waiting = [item for item in waiting if item not in taken]
+        fills.append([item[1:] for item in taken])
+    return fills + [[], [], []]
+
+
+def tile_dynamicattention4_pa_v_kernel(tc, q, src, trg, Ws, b_s, Wt, b_t, s_key, t_key, grad_out,
+                                                    out_0, out_1):
     nc = tc.nc
     with ExitStack() as ctx:
         sb = ctx.enter_context(tc.tile_pool(name="sb", bufs=1))
         ps = ctx.enter_context(tc.psum_pool(name="ps", bufs=1))
         ctx.enter_context(tc.manual_schedule())
 
-        trg_rows = trg.rearrange("b t f -> (b t) f").rearrange("(p j) f -> p j f", j=PACK)
-
-        def source(job):
-            kind, a, c = job
-            cols = slice(c * BANK, (c + 1) * BANK)
-            if kind == "g":
-                return grad_out[a].rearrange("(p j) t s -> p j (t s)", j=PACK)[:, :, cols]
-            if kind == "q":
-                return q[a].rearrange("(p j) h -> p j h", j=PACK)[:, :, cols]
-            return trg_rows[:, :, cols]
-
-        head_jobs = [("q", 0, 0)] + [("g", 0, c) for c in range(4)]
-        jobs = []
-        for b in range(1, B):
-            jobs = jobs + [("q", b - 1, 1)] + [("g", b, c) for c in range(4)] + [("q", b, 0)]
-        jobs = jobs + [("q", B - 1, 1), ("x", 0, 0), ("x", 0, 1)]
-        pieces = [(job, h) for job in jobs for h in range(2)]
-        counts = [2, 2, 2, 1, 2, 2, 1] + [2, 1] * 8 + [1, 2, 1, 1, 1] + [0] * 4
-        starts = [sum(counts[:n]) for n in range(UNITS + 1)]
-        step_pieces = [pieces[starts[n]:starts[n + 1]] for n in range(UNITS)]
-
-        raw, inter, codes = {}, {}, {}
-        code_bufs = {"g": 8, "q": 4, "x": 2}
-
-        def load(job):
-            raw[job] = sb.tile([P, PACK, BANK], BF16, name="raw", bufs=6)
-            nc.sync.dma_start(out=raw[job][:], in_=source(job))
-
-        def interleave_v(dst, rows):
-            nc.vector.tensor_copy(out=dst, in_=rows.rearrange("p j c -> p c j"))
-
-        def interleave_g(dst, rows):
-            nc.gpsimd.tensor_scalar(out=dst, in0=rows.rearrange("p j c -> p c j"), scalar1=1.0, scalar2=1.0,
-                                    op0=ALU.mult, op1=ALU.mult)
-
-        def chain_tile(h):
-            chain = sb.tile([P, HALF, PACK], BF16, name="chain%d" % h, bufs=1, align_bytes=64)
-            return chain
-
-        def quantize(job, h, tile):
-            kind = job[0]
-            if h == 0:
-                words = sb.tile([P, BANK], U32, name="words_" + kind, bufs=code_bufs[kind], align_bytes=64)
-                scales = sb.tile([P, BANK], U8, name="scales_" + kind, bufs=code_bufs[kind], align_bytes=64)
-                codes[job] = (words, scales)
-            cols = slice(h * HALF, h * HALF + tile.shape[1])
-            nc.vector.quantize_mx(out=codes[job][0][:, cols].bitcast(E5 if kind == "g" else E4),
-                                  scales=codes[job][1][:, cols], in_=tile.rearrange("p c j -> p (c j)"))
-
-        def mx(out, lhs, lhs_cols, lhs_fmt, rhs, rhs_cols, rhs_fmt, start, stop):
-            nc.tensor.matmul_mx(out=out, lhsT=lhs[0][:, lhs_cols].bitcast(lhs_fmt), lhsT_scale=lhs[1][:, lhs_cols],
-                                rhs=rhs[0][:, rhs_cols].bitcast(rhs_fmt), rhs_scale=rhs[1][:, rhs_cols],
-                                start=start, stop=stop)
+        def drel_bank():
+            return ps.tile([P, BANK], F32, name="drel_bank", bufs=UNIT_BANKS)
 
         def spare_bank():
-            spare = ps.tile([P, BANK], F32, name="spare", bufs=2)
-            return spare
+            return ps.tile([P, BANK], F32, name="spare_bank", bufs=2)
 
-        def score_bank():
-            score = ps.tile([P, BANK], F32, name="score", bufs=4)
-            return score
+        def mx_pair(name, width, bufs=1):
+            words = sb.tile([P, width], U32, name=name + "_words", bufs=bufs, align_bytes=64)
+            scales = sb.tile([P, width], U8, name=name + "_scales", bufs=bufs, align_bytes=64)
+            return words, scales
+
+        def quantize(pair, fmt, lo, values):
+            cols = slice(lo, lo + values.shape[1] // PACK)
+            nc.vector.quantize_mx(out=pair[0][:, cols].bitcast(fmt), scales=pair[1][:, cols], in_=values)
+
+        def matmul_mx(bank, still, still_lo, still_fmt, moving, moving_lo, moving_fmt, start=True, stop=True):
+            m_cols, n_cols = slice(still_lo, still_lo + P), slice(moving_lo, moving_lo + BANK)
+            nc.tensor.matmul_mx(out=bank[:], lhsT=still[0][:, m_cols].bitcast(still_fmt), lhsT_scale=still[1][:, m_cols],
+                                rhs=moving[0][:, n_cols].bitcast(moving_fmt), rhs_scale=moving[1][:, n_cols],
+                                start=start, stop=stop)
+
+        raw, codes = {}, {}
+        code_bufs = {"g": 2 * UNIT_BANKS, "q": 4, "trg": 2}
+
+        def load_slab(slab):
+            tensor, b, block = slab
+            if tensor == "g":
+                rows = grad_out[b].rearrange("(p j) t s -> p j (t s)", j=PACK)
+            elif tensor == "q":
+                rows = q[b].rearrange("(p j) h -> p j h", j=PACK)
+            else:
+                rows = trg.rearrange("b t f -> (b t) f").rearrange("(p j) f -> p j f", j=PACK)
+            raw[slab] = sb.tile([P, PACK, BANK], BF16, name="raw", bufs=2 * LOAD_AHEAD)
+            nc.sync.dma_start(out=raw[slab][:], in_=rows[:, :, block * BANK:(block + 1) * BANK])
+
+        def piece_tile(n):
+            return sb.tile([P, PIECE, PACK], BF16, name="piece%d" % n, bufs=1, align_bytes=64)
+
+        def interleave_vector(grouped, rows):
+            nc.vector.tensor_copy(out=grouped, in_=rows.rearrange("p j c -> p c j"))
+
+        def interleave_gpsimd(grouped, rows):
+            nc.gpsimd.tensor_scalar(out=grouped, in0=rows.rearrange("p j c -> p c j"), scalar1=1.0, scalar2=1.0,
+                                    op0=ALU.mult, op1=ALU.mult)
+
+        def flat(grouped):
+            return grouped[:].rearrange("p c j -> p (c j)")
+
+        def quantize_slab(slab, lo, grouped):
+            if lo == 0:
+                codes[slab] = mx_pair(slab[0], BANK, code_bufs[slab[0]])
+            quantize(codes[slab], E5M2 if slab[0] == "g" else E4M3, lo, flat(grouped))
+
+        first_slabs = [("q", 0, 0)] + [("g", 0, a) for a in range(UNIT_BANKS)]
+        slabs = []
+        for b in range(1, B):
+            slabs = slabs + [("q", b - 1, 1)] + [("g", b, a) for a in range(UNIT_BANKS)] + [("q", b, 0)]
+        slabs = slabs + [("q", B - 1, 1), ("trg", 0, 0), ("trg", 0, 1)]
+        pieces = [(slab, lo) for slab in slabs for lo in (0, PIECE)]
+        per_b = 2 * (UNIT_BANKS + 2)
+        piece_counts = spread(per_b, 2 * GROUP - 1) + spread(per_b, 2 * GROUP) * (B - 2)
+        last_b_from = len(piece_counts)
+        piece_counts = piece_counts + spread(len(pieces) - sum(piece_counts), CLOSING + 1 - last_b_from)
+        piece_counts = piece_counts + [0] * (UNITS - len(piece_counts))
+        piece_starts = [sum(piece_counts[:n]) for n in range(UNITS + 1)]
+        fills = plan_fills(piece_counts, last_b_from)
 
         t_rows, t_cols = {}, {}
 
         def load_t(k):
-            b, half = GROUPS[k]
+            b, half = divmod(k, 2)
             t_rows[k] = sb.tile([P, BANK], F32, name="t_rows", bufs=2)
             nc.sync.dma_start(out=t_rows[k][:], in_=t_key[b][:, half * BANK:(half + 1) * BANK])
 
-        def transpose4(rows):
+        def transpose_blocks(rows):
             bank = spare_bank()
-            for c in range(4):
+            for c in range(GROUP):
                 nc.tensor.transpose(bank[:, c * P:(c + 1) * P], rows[:, c * P:(c + 1) * P], ident[:])
             return bank
 
@@ -123,100 +151,109 @@ def tile_dynamicattention4_pa_v_kernel(tc, q, src, trg, Ws, b_s, Wt, b_t, s_key,
             t_cols[k] = sb.tile([P, BANK], F32, name="t_cols", bufs=3)
             nc.vector.tensor_copy(out=t_cols[k][:], in_=bank[:])
 
-        rel, score, prod, dz_sum, dz_rows = {}, {}, {}, {}, {}
+        rel, drel, weighted, dz_sum, dz_rows = {}, {}, {}, {}, {}
 
         def tanh(u, s_lo, s_hi):
-            b, half = GROUPS[u // 4]
-            c = u % 4
+            k, c = divmod(u, GROUP)
+            b, half = divmod(k, 2)
             if s_lo == 0:
-                rel[u] = sb.tile([P, 4, S, TQ], F32, name="rel", bufs=AHEAD + 1)
+                rel[u] = sb.tile([P, S, T], F32, name="rel", bufs=AHEAD + 1)
             for s in range(s_lo, s_hi):
                 col = c * P + 2 * (b * S + s) + half
-                nc.scalar.activation(out=rel[u][:, :, s, :],
-                                     in_=t_cols[u // 4][:, c * P:(c + 1) * P].rearrange("p (a t) -> p a t", a=4),
-                                     func=ACT.Tanh, bias=s_cols[:, col:col + 1])
+                nc.scalar.activation(out=rel[u][:, s, :], in_=t_cols[k][:, c * P:(c + 1) * P], func=ACT.Tanh,
+                                     bias=s_cols[:, col:col + 1])
 
-        def columns(u, lo, hi):
-            return rel[u][:].rearrange("p a s t -> p (a s t)")[:, lo:hi]
-
-        def shares(u):
+        def square_shares(u):
             step = u - 1
-            if step < 0:
-                return UNIT_COLS, UNIT_COLS
-            n = counts[step]
-            gp = 0 if n == 2 or step >= 30 else (GP_SQ_SINGLE if step < 23 else GP_SQ_LATE)
-            ve = (V_SQ_DOUBLE if n == 2 else (V_SQ_SINGLE if step < 23 else V_SQ_LATE)) if V_SQ_FROM <= step < V_SQ_TO else 0
-            return UNIT_COLS - gp - ve, UNIT_COLS - gp
+            on_gpsimd, on_vector = 0, 0
+            if step >= 1:
+                one_piece = piece_counts[step] < 2
+                on_vector = VECTOR_SQUARES_ONE_PIECE if one_piece and step < last_b_from else VECTOR_SQUARES
+                if one_piece and step < UNITS - 2:
+                    on_gpsimd = GPSIMD_SQUARES if step < last_b_from else GPSIMD_SQUARES_LAST_B
+            return S * T - on_gpsimd - on_vector, S * T - on_gpsimd
 
-        def square_s(u):
-            part = columns(u, 0, shares(u)[0])
+        def rel_columns(u, lo, hi):
+            return rel[u][:].rearrange("p s t -> p (s t)")[:, lo:hi]
+
+        def square_scalar(u):
+            part = rel_columns(u, 0, square_shares(u)[0])
             nc.scalar.activation(out=part, in_=part, func=ACT.Square, bias=zero[:])
 
-        def square_v(u):
-            lo, hi = shares(u)
+        def square(engine, u, lo, hi):
             if hi > lo:
-                part = columns(u, lo, hi)
-                nc.vector.tensor_tensor(out=part, in0=part, in1=part, op=ALU.mult)
+                part = rel_columns(u, lo, hi)
+                engine.tensor_tensor(out=part, in0=part, in1=part, op=ALU.mult)
 
-        def square_g(u):
-            lo = shares(u)[1]
-            if lo < UNIT_COLS:
-                part = columns(u, lo, UNIT_COLS)
-                nc.gpsimd.tensor_tensor(out=part, in0=part, in1=part, op=ALU.mult)
+        def scalar_step(u):
+            if u < UNITS:
+                tanh(u, 0, 2)
+            if u - 1 < UNITS:
+                square_scalar(u - 1)
+            if u < UNITS:
+                tanh(u, 2, S)
 
-        def score_mx(u, a):
-            b, half = GROUPS[u // 4]
-            c = u % 4
-            score[u, a] = score_bank()
-            mx(score[u, a][:], codes["q", b, half], slice(c * P, (c + 1) * P), E4,
-               codes["g", b, a], slice(0, BANK), E5, True, True)
+        def drel_product(u, a):
+            k, c = divmod(u, GROUP)
+            b, half = divmod(k, 2)
+            drel[u, a] = drel_bank()
+            matmul_mx(drel[u, a], codes["q", b, half], c * P, E4M3, codes["g", b, a], 0, E5M2)
 
         def weigh(u, a):
             if a == 0:
-                prod[u] = sb.tile([P, S, T], F32, name="prod", bufs=3)
-            nc.vector.scalar_tensor_tensor(out=prod[u][:, :, a * TQ:(a + 1) * TQ], in0=rel[u][:, a, :, :], scalar=1.0,
-                                           in1=score[u, a][:].rearrange("p (t s) -> p s t", s=S),
+                weighted[u] = sb.tile([P, S, T], F32, name="weighted", bufs=3)
+            tokens = slice(a * BANK_TOKENS, (a + 1) * BANK_TOKENS)
+            nc.vector.scalar_tensor_tensor(out=weighted[u][:, :, tokens], in0=rel[u][:, :, tokens], scalar=1.0,
+                                           in1=drel[u, a][:].rearrange("p (t s) -> p s t", s=S),
                                            op0=ALU.subtract, op1=ALU.mult)
 
-        def sum_s(u, lo, hi):
-            if lo == 0:
+        def sum_over_s(u, s_lo, s_hi):
+            if s_lo == 0:
                 dz_sum[u] = ps.tile([P, P], F32, name="dz_sum", bufs=2)
-            for s in range(lo, hi):
-                nc.tensor.matmul(out=dz_sum[u][:], lhsT=prod[u][:, s, :], rhs=ident[:], is_transpose=(s not in WARM or u >= 29),
-                                 start=(s == 0), stop=(s == S - 1))
+            for s in range(s_lo, s_hi):
+                nc.tensor.matmul(out=dz_sum[u][:], lhsT=weighted[u][:, s, :], rhs=ident[:],
+                                 is_transpose=(s not in PLAIN_S or u >= UNITS - 3), start=(s == 0), stop=(s == S - 1))
 
         def round_dz(u):
-            k, c = divmod(u, 4)
+            k, c = divmod(u, GROUP)
             if c == 0:
                 dz_rows[k] = sb.tile([P, BANK], BF16, name="dz_rows", bufs=3)
-            nc.vector.tensor_scalar(out=dz_rows[k][:, c * P:(c + 1) * P], in0=dz_sum[u][:], scalar1=-1.0 / 32.0,
-                                    scalar2=None, op0=ALU.mult)
+            nc.vector.tensor_scalar(out=dz_rows[k][:, c * P:(c + 1) * P], in0=dz_sum[u][:],
+                                    scalar1=-1.0 / math.sqrt(H), scalar2=None, op0=ALU.mult)
 
         def regroup(k, lo, hi):
-            b, half = GROUPS[k]
+            b, half = divmod(k, 2)
+            rows = slice(b * T // PACK, (b + 1) * T // PACK)
             for j in range(PACK):
-                nc.sync.dma_start(out=z_rows[half][32 * b:32 * (b + 1), j, lo:hi], in_=dz_rows[k][j::PACK, lo:hi])
+                nc.sync.dma_start(out=dz_slabs[half][rows, j, lo:hi], in_=dz_rows[k][j::PACK, lo:hi])
 
-        def finish(u):
+        def round_and_regroup(u):
+            k, c = divmod(u, GROUP)
             round_dz(u)
-            if u < 24 and u % 4 == 3:
-                regroup(u // 4, 0, BANK)
-            if u >= 24 and u % 4 == 1:
-                regroup(u // 4, 0, HALF)
-            if u >= 24 and u % 4 == 2:
-                regroup(u // 4, HALF, HALF + P)
+            if k < GROUPS - 2 and c == GROUP - 1:
+                regroup(k, 0, BANK)
+            if k >= GROUPS - 2 and c == 1:
+                regroup(k, 0, PIECE)
+            if k >= GROUPS - 2 and c == 2:
+                regroup(k, PIECE, PIECE + P)
 
         def pick_rows(k):
             bank = spare_bank()
             for j in range(PACK):
-                nc.tensor.matmul(out=bank[:, j * P:(j + 1) * P], lhsT=pick[:, j, :], rhs=dz_rows[k][:, HALF + P:BANK],
+                nc.tensor.matmul(out=bank[:, j * P:(j + 1) * P], lhsT=pick[:, j, :], rhs=dz_rows[k][:, BANK - P:BANK],
                                  start=True, stop=True)
             return bank
 
-        def take_picked(tile, bank):
-            nc.vector.tensor_copy(out=tile[96:P, P:HALF, :], in_=bank[96:P, :].rearrange("p (j c) -> p c j", j=PACK))
+        def take_picked(grouped, bank):
+            nc.vector.tensor_copy(out=grouped[LAST_ROWS:P, P:PIECE, :],
+                                  in_=bank[LAST_ROWS:P, :].rearrange("p (j c) -> p c j", j=PACK))
 
-        w_rows = {}
+        def transpose_words(bank, block, words):
+            for e in range(2):
+                cols = slice((2 * block + e) * P, (2 * block + e + 1) * P)
+                nc.tensor.transpose(bank[:, cols], words[:, e::2], ident[:])
+
+        w_rows, dz_pairs, dz_codes = {}, {}, {}
 
         def load_w(i):
             w_rows[i] = sb.tile([P, H], BF16, name="w_rows", bufs=4)
@@ -224,87 +261,69 @@ def tile_dynamicattention4_pa_v_kernel(tc, q, src, trg, Ws, b_s, Wt, b_t, s_key,
 
         def transpose_w(i):
             bank = spare_bank()
-            words = w_rows[i][:].bitcast(F32)
             for g in range(2):
-                for e in range(2):
-                    n = 2 * g + e
-                    nc.tensor.transpose(bank[:, n * P:(n + 1) * P], words[:, 256 * g + e:256 * (g + 1):2], ident[:])
+                transpose_words(bank, g, w_rows[i][:, g * BANK:(g + 1) * BANK].bitcast(F32))
             return bank
 
         def take_w(i, bank):
-            nc.vector.tensor_copy(out=w_pairs[:].rearrange("p (g f e) -> p g f e", g=2, e=2)[:, :, i * P:(i + 1) * P, :],
+            pairs = w_pairs[:].rearrange("p (g f e) -> p g f e", g=2, e=2)
+            nc.vector.tensor_copy(out=pairs[:, :, i * P:(i + 1) * P, :],
                                   in_=bank[:].rearrange("p (g e f) -> p g f e", g=2, e=2))
 
-        def quantize_w(n):
-            cols = slice(n * BANK, (n + 1) * BANK)
-            nc.vector.quantize_mx(out=w_codes[0][:, cols].bitcast(E4), scales=w_codes[1][:, cols],
-                                  in_=w_pairs[:, n * 2 * BANK:(n + 1) * 2 * BANK].bitcast(BF16))
+        def quantize_w(g, n):
+            lo = g * F + n * BANK
+            quantize(w_codes, E4M3, lo, w_pairs[:, 2 * lo:2 * (lo + BANK)].bitcast(BF16))
 
-        y_pairs, y_codes = {}, {}
-
-        def transpose_y(k):
+        def transpose_dz(k):
             bank = spare_bank()
-            words = dz_rows[k][:].bitcast(F32)
-            for e in range(2):
-                nc.tensor.transpose(bank[:, e * P:(e + 1) * P], words[:, e:2 * P:2], ident[:])
+            transpose_words(bank, 0, dz_rows[k][:].bitcast(F32))
             return bank
 
-        def take_y(k, bank):
-            y_pairs[k] = sb.tile([P, 2 * P], F32, name="y_pairs", bufs=2, align_bytes=64)
-            nc.vector.tensor_copy(out=y_pairs[k][:].rearrange("p (t e) -> p t e", e=2),
-                                  in_=bank[:, 0:2 * P].rearrange("p (e t) -> p t e", e=2))
+        def take_dz(k, bank):
+            dz_pairs[k] = sb.tile([P, 2 * T], F32, name="dz_pairs", bufs=2, align_bytes=64)
+            nc.vector.tensor_copy(out=dz_pairs[k][:].rearrange("p (t e) -> p t e", e=2),
+                                  in_=bank[:, 0:2 * T].rearrange("p (e t) -> p t e", e=2))
 
-        def quantize_y(k):
-            words = sb.tile([P, P], U32, name="y_words", bufs=8, align_bytes=64)
-            scales = sb.tile([P, P], U8, name="y_scales", bufs=8, align_bytes=64)
-            nc.vector.quantize_mx(out=words[:].bitcast(E5), scales=scales[:], in_=y_pairs[k][:].bitcast(BF16))
-            y_codes[GROUPS[k]] = (words, scales)
+        def quantize_dz(k):
+            dz_codes[k] = mx_pair("dz_features", T, GROUPS)
+            quantize(dz_codes[k], E5M2, 0, dz_pairs[k][:].bitcast(BF16))
 
-        def out0_mx(b, n, bank):
+        def out_0_product(b, n, bank):
             for g in range(2):
-                mx(bank[:], y_codes[b, g], slice(0, P), E5, w_codes, slice(g * F + n * BANK, g * F + (n + 1) * BANK), E4,
-                   g == 0, g == 1)
+                matmul_mx(bank, dz_codes[2 * b + g], 0, E5M2, w_codes, g * F + n * BANK, E4M3, g == 0, g == 1)
             return bank
 
-        def out1_mx(i, end, bank):
-            c = i % 4
-            mx(bank[:], codes["x", 0, i // 4], slice(c * P, (c + 1) * P), E4, z_codes, slice(end - BANK, end), E5,
-               True, True)
+        def out_1_product(i, half, bank, back=0):
+            block, c = divmod(i, GROUP)
+            matmul_mx(bank, codes["trg", 0, block], c * P, E4M3, dz_token_codes, half * BANK - back, E5M2)
             return bank
 
-        def store0(copy, b, n, bank):
-            result = sb.tile([P, BANK], F32, name="result", bufs=8)
-            copy(out=result[:], in_=bank[:])
-            nc.sync.dma_start(out=out_0[b][:, n * BANK:(n + 1) * BANK], in_=result[:])
+        def store(copy, bank, rows):
+            width = rows.shape[1]
+            result = sb.tile([P, width], F32, name="result", bufs=10)
+            copy(out=result[:], in_=bank[:, BANK - width:BANK])
+            nc.sync.dma_start(out=rows, in_=result[:])
 
-        def store0x(copy, i, bank):
-            result = sb.tile([P, BANK], F32, name="result", bufs=8)
-            copy(out=result[:], in_=bank[:])
-            nc.sync.dma_start(out=out_1[i * P:(i + 1) * P, BANK:H], in_=result[:])
+        def store_out_0(copy, b, n, bank):
+            store(copy, bank, out_0[b][:, n * BANK:(n + 1) * BANK])
 
-        wide = {}
+        result_pairs = {}
 
-        def store1(copy, i, lo, end, bank, queue=nc.scalar):
-            width = end - lo
-            count = 2 * BANK // width
-            first = i - i % count
-            if i == first:
-                wide[lo] = sb.tile([P, count, width], F32, name="wide", bufs=4)
-            copy(out=wide[lo][:, i - first, :], in_=bank[:, BANK - width:BANK])
-            if i == first + count - 1:
-                rows = out_1[first * P:(first + count) * P, lo:end].rearrange("(n p) c -> p n c", p=P)
-                queue.dma_start(out=rows, in_=wide[lo][:])
-
-        def quantize_z(tile, lo, hi):
-            nc.vector.quantize_mx(out=z_codes[0][:, lo:hi].bitcast(E5), scales=z_codes[1][:, lo:hi],
-                                  in_=tile[:, 0:hi - lo, :].rearrange("p c j -> p (c j)"))
+        def out_1_first_half(i, bank):
+            pair, n = divmod(i, 2)
+            out_1_product(i, 0, bank)
+            if n == 0:
+                result_pairs[pair] = sb.tile([P, 2, BANK], F32, name="result_pair", bufs=3)
+            nc.scalar.copy(out=result_pairs[pair][:, n, :], in_=bank[:])
+            if n == 1:
+                rows = out_1[2 * pair * P:2 * (pair + 1) * P, 0:BANK].rearrange("(n p) h -> p n h", p=P)
+                nc.scalar.dma_start(out=rows, in_=result_pairs[pair][:])
 
         load_t(0)
         s_rows = sb.tile([P, BANK], F32, name="s_rows")
-        nc.sync.dma_start(out=s_rows[:], in_=s_key.rearrange("b s (u h) -> (b s u) h", u=2))
-        for job in head_jobs:
-            load(job)
-        load(jobs[0])
+        nc.sync.dma_start(out=s_rows[:], in_=s_key.rearrange("b s (half h) -> (b s half) h", half=2))
+        for slab in first_slabs + slabs[:1]:
+            load_slab(slab)
         load_t(1)
 
         ident = sb.tile([P, P], F32, name="ident")
@@ -313,166 +332,162 @@ def tile_dynamicattention4_pa_v_kernel(tc, q, src, trg, Ws, b_s, Wt, b_t, s_key,
         nc.vector.memset(seed[:], 0.0)
         zero = sb.tile([P, 1], F32, name="zero")
         nc.scalar.activation(out=zero[:], in_=seed[:], func=ACT.Tanh, bias=seed[:])
-
-        w_pairs = sb.tile([P, 2 * 2 * F], F32, name="w_pairs", align_bytes=64)
-        w_words = sb.tile([P, 2 * F], U32, name="w_words", align_bytes=64)
-        w_scales = sb.tile([P, 2 * F], U8, name="w_scales", align_bytes=64)
-        w_codes = (w_words, w_scales)
-        z_words = sb.tile([P, H], U32, name="z_words", align_bytes=64)
-        z_scales = sb.tile([P, H], U8, name="z_scales", align_bytes=64)
-        z_codes = (z_words, z_scales)
-        z_rows0 = sb.tile([P, PACK, BANK], BF16, name="z_rows0")
-        z_rows1 = sb.tile([P, PACK, BANK], BF16, name="z_rows1")
-        z_rows = (z_rows0, z_rows1)
-
         pick = sb.tile([P, PACK, P], BF16, name="pick")
         nc.gpsimd.memset(pick[:], 0.0)
-        nc.gpsimd.tensor_copy(out=pick[:, :, 96:P], in_=ident[:].rearrange("p (i j) -> p j i", j=PACK))
-        t_bank = transpose4(t_rows[0])
-        s_bank = transpose4(s_rows)
+        nc.gpsimd.tensor_copy(out=pick[:, :, LAST_ROWS:P], in_=ident[:].rearrange("p (i j) -> p j i", j=PACK))
+
+        w_pairs = sb.tile([P, 2 * F * 2], F32, name="w_pairs", align_bytes=64)
+        w_codes = mx_pair("w", 2 * F)
+        dz_token_codes = mx_pair("dz_tokens", H)
+        dz_slabs = [sb.tile([P, PACK, BANK], BF16, name="dz_slab%d" % half) for half in range(2)]
+
+        t_bank = transpose_blocks(t_rows[0])
+        s_bank = transpose_blocks(s_rows)
         take_t(0, t_bank)
         s_cols = sb.tile([P, BANK], F32, name="s_cols")
         nc.vector.tensor_copy(out=s_cols[:], in_=s_bank[:])
 
-        for n, job in enumerate(head_jobs[:-1]):
-            inter[job] = sb.tile([P, BANK, PACK], BF16, name="head", bufs=2, align_bytes=64)
-            interleave_v(inter[job][:], raw[job][:])
-            if n > 0:
-                quantize(head_jobs[n - 1], 0, inter[head_jobs[n - 1]][:])
-        job = head_jobs[-1]
-        for h in range(2):
-            inter[job, h] = chain_tile(h)
-            interleave_v(inter[job, h][:], raw[job][:, :, h * HALF:(h + 1) * HALF])
-        quantize(head_jobs[-2], 0, inter[head_jobs[-2]][:])
-        for h in range(2):
-            quantize(job, h, inter[job, h][:])
+        waiting = None
+        for slab in first_slabs[:-1]:
+            grouped = sb.tile([P, BANK, PACK], BF16, name="first_grouped", bufs=2, align_bytes=64)
+            interleave_vector(grouped[:], raw[slab][:])
+            if waiting is not None:
+                quantize_slab(*waiting)
+            waiting = (slab, 0, grouped)
+        slab = first_slabs[-1]
+        halves = [(slab, n * PIECE, piece_tile(n)) for n in range(2)]
+        for slab, lo, grouped in halves:
+            interleave_vector(grouped[:], raw[slab][:, :, lo:lo + PIECE])
+        for item in [waiting] + halves:
+            quantize_slab(*item)
+
         loaded = LOAD_AHEAD
-        for n in range(1, loaded):
-            load(jobs[n])
-        for i in range(4):
+        for slab in slabs[1:loaded]:
+            load_slab(slab)
+        for kind, i in fills[0] + fills[1]:
             load_w(i)
-        for a in range(4):
-            score_mx(0, a)
-        t_bank = transpose4(t_rows[1])
+        for a in range(UNIT_BANKS):
+            drel_product(0, a)
+        filled = [("t", 1, transpose_blocks(t_rows[1]))]
         tanh(0, 0, S)
         for u in range(1, AHEAD):
-            tanh(u, 0, 2)
-            square_s(u - 1)
-            tanh(u, 2, S)
+            scalar_step(u)
 
-        wq_steps = {3: 0, 6: 2, 10: 1, 12: 3}
-        fills = {0: [("w", 0), ("w", 1)], 1: [("w", 2), ("w", 3)], 3: [("t", 2), ("w", 4)], 4: [("w", 5), ("w", 6)],
-                 6: [("t", 3), ("y", 0)], 8: [("w", 7)], 10: [("t", 4), ("y", 1)], 12: [("o0", (0, 0))],
-                 14: [("t", 5), ("y", 2)], 16: [("o0", (0, 1))], 18: [("t", 6), ("y", 3)],
-                 20: [("o0", (1, 0)), ("o0", (1, 1))], 23: [("t", 7), ("y", 4)], 25: [("y", 5)],
-                 26: [("o0", (2, 0))], 27: [("o0", (2, 1))], 29: [("y", 6)]}
-        filled = [("t", 1, t_bank)]
+        one_piece_steps = [step for step in range(last_b_from) if piece_counts[step] == 1]
+        w_done = [1 + max(step for step in range(UNITS) for kind, i in fills[step] if kind == "w" and i // GROUP == n)
+                  for n in range(2)]
+        w_steps = {}
+        for n in range(2):
+            for g, step in enumerate([step for step in one_piece_steps if step > w_done[n]][:2]):
+                w_steps[step] = (g, n)
+
         for step in range(UNITS):
             last = step == UNITS - 1
-            while loaded < len(jobs) and 2 * loaded < starts[min(step + LOAD_AHEAD + 1, UNITS)]:
-                load(jobs[loaded])
+            while loaded < len(slabs) and 2 * loaded < piece_starts[min(step + LOAD_AHEAD + 1, UNITS)]:
+                load_slab(slabs[loaded])
                 loaded = loaded + 1
-            for kind, arg in fills.get(step + 2, []):
+            for kind, i in fills[step + 2]:
                 if kind == "w":
-                    load_w(arg)
+                    load_w(i)
                 if kind == "t":
-                    load_t(arg)
-            for n, (job, h) in enumerate(step_pieces[step]):
-                inter[job, h] = chain_tile(n)
-                interleave_g(inter[job, h][:], raw[job][:, :, h * HALF:(h + 1) * HALF])
-            z_tiles = []
-            if last:
-                z_last = chain_tile(1)
-            for lo in {28: (0,), 31: (BANK,)}.get(step, ()):
-                z_tile = chain_tile(0)
-                interleave_g(z_tile[:], z_rows[lo // BANK][:, :, 0:HALF])
-                z_tiles.append((z_tile, lo))
-            if step == 29:
-                z_tile = chain_tile(0)
-                interleave_g(z_tile[0:96, P:HALF, :], z_rows[0][0:96, :, HALF + P:BANK])
-                interleave_g(z_tile[:, 0:P, :], z_rows[0][:, :, HALF:HALF + P])
-                z_tiles.append((z_tile, HALF))
-                filled.append(("pick", z_tile, pick_rows(6)))
+                    load_t(i)
+
+            grouped_pieces = []
+            for n, (slab, lo) in enumerate(pieces[piece_starts[step]:piece_starts[step + 1]]):
+                grouped = piece_tile(n)
+                interleave_gpsimd(grouped[:], raw[slab][:, :, lo:lo + PIECE])
+                grouped_pieces.append((slab, lo, grouped))
+            dz_piece = None
+            if step == CLOSING + 1 or last:
+                half = int(last)
+                dz_piece = (half * BANK, piece_tile(0))
+                interleave_gpsimd(dz_piece[1][:], dz_slabs[half][:, :, 0:PIECE])
+            if step == CLOSING + 2:
+                dz_piece = (PIECE, piece_tile(0))
+                interleave_gpsimd(dz_piece[1][0:LAST_ROWS, P:PIECE, :], dz_slabs[0][0:LAST_ROWS, :, BANK - P:BANK])
+                interleave_gpsimd(dz_piece[1][:, 0:P, :], dz_slabs[0][:, :, PIECE:PIECE + P])
+                filled.append(("picked", dz_piece[1], pick_rows(GROUPS - 2)))
             if not last:
-                square_g(step + 1)
-            if step + AHEAD < UNITS:
-                tanh(step + AHEAD, 0, 2)
-            if step + AHEAD - 1 < UNITS:
-                square_s(step + AHEAD - 1)
-            if step + AHEAD < UNITS:
-                tanh(step + AHEAD, 2, S)
+                square(nc.gpsimd, step + 1, square_shares(step + 1)[1], S * T)
+
+            scalar_step(step + AHEAD)
+
             for a in (0, 1):
                 weigh(step, a)
                 if last:
-                    store1(nc.scalar.copy, 4 + a, 0, BANK, out1_mx(4 + a, BANK, score_bank()))
+                    out_1_first_half(4 + a, drel_bank())
                 else:
-                    score_mx(step + 1, a)
+                    drel_product(step + 1, a)
             if step > 0:
-                sum_s(step - 1, SPLIT, S)
-            if 2 <= step < 28:
-                finish(step - 2)
+                sum_over_s(step - 1, S // 2, S)
+            if 2 <= step <= CLOSING:
+                round_and_regroup(step - 2)
             if step == UNITS - 2:
                 for i in (0, 1):
-                    store1(nc.scalar.copy, i, 0, BANK, out1_mx(i, BANK, spare_bank()))
+                    out_1_first_half(i, spare_bank())
             for a in (2, 3):
                 weigh(step, a)
                 if not last:
-                    score_mx(step + 1, a)
-            quantize_late = []
-            for kind, arg, bank in filled:
+                    drel_product(step + 1, a)
+            dz_taken = []
+            for kind, i, bank in filled:
                 if kind == "t":
-                    take_t(arg, bank)
+                    take_t(i, bank)
                 if kind == "w":
-                    take_w(arg, bank)
-                if kind == "y":
-                    take_y(arg, bank)
-                    quantize_late.append(arg)
-                if kind == "pick":
-                    take_picked(arg, bank)
-                if kind == "o0":
-                    store0(nc.vector.tensor_copy, arg[0], arg[1], bank)
-            filled = []
-            sum_s(step, 0, S if last else SPLIT)
+                    take_w(i, bank)
+                if kind == "dz":
+                    take_dz(i, bank)
+                    dz_taken.append(i)
+                if kind == "picked":
+                    take_picked(i, bank)
+                if kind == "out_0":
+                    store_out_0(nc.vector.tensor_copy, *i, bank)
+            sum_over_s(step, 0, S if last else S // 2)
             if step == UNITS - 2:
                 for i in (2, 3):
-                    store1(nc.scalar.copy, i, 0, BANK, out1_mx(i, BANK, spare_bank()))
-            if not last:
-                square_v(step + 1)
-            for k in quantize_late:
-                quantize_y(k)
-            if step in wq_steps:
-                quantize_w(wq_steps[step])
-            for job, h in step_pieces[step]:
-                quantize(job, h, inter[job, h][:])
-            if last:
-                finish(step - 1)
-                interleave_v(z_last[0:96, P:HALF, :], z_rows[1][0:96, :, HALF + P:BANK])
-                round_dz(step)
-            for z_tile, lo in z_tiles:
-                quantize_z(z_tile, lo, lo + HALF)
-            if 27 <= step < UNITS - 1:
-                finish(step - 1)
-            for kind, arg in fills.get(step, []):
-                if kind == "t":
-                    filled.append((kind, arg, transpose4(t_rows[arg])))
-                if kind == "w":
-                    filled.append((kind, arg, transpose_w(arg)))
-                if kind == "y":
-                    filled.append((kind, arg, transpose_y(arg)))
-                if kind == "o0":
-                    filled.append((kind, arg, out0_mx(arg[0], arg[1], spare_bank())))
+                    out_1_first_half(i, spare_bank())
 
-        copies = (nc.scalar.copy, nc.vector.tensor_copy)
+            if not last:
+                square(nc.vector, step + 1, *square_shares(step + 1))
+            for k in dz_taken:
+                quantize_dz(k)
+            if step in w_steps:
+                quantize_w(*w_steps[step])
+            for item in grouped_pieces:
+                quantize_slab(*item)
+            if last:
+                round_and_regroup(step - 1)
+                last_piece = piece_tile(1)
+                interleave_vector(last_piece[0:LAST_ROWS, P:PIECE, :], dz_slabs[1][0:LAST_ROWS, :, BANK - P:BANK])
+                round_dz(step)
+            if dz_piece is not None:
+                quantize(dz_token_codes, E5M2, dz_piece[0], flat(dz_piece[1]))
+            if CLOSING <= step < UNITS - 1:
+                round_and_regroup(step - 1)
+
+            filled = []
+            for kind, i in fills[step]:
+                if kind == "t":
+                    filled.append((kind, i, transpose_blocks(t_rows[i])))
+                if kind == "w":
+                    filled.append((kind, i, transpose_w(i)))
+                if kind == "dz":
+                    filled.append((kind, i, transpose_dz(i)))
+                if kind == "out_0":
+                    filled.append((kind, i, out_0_product(*i, spare_bank())))
+
         for i in (6, 7):
-            store1(nc.scalar.copy, i, 0, BANK, out1_mx(i, BANK, score_bank()))
-        picked = pick_rows(7)
-        y_bank = transpose_y(7)
-        take_picked(z_last, picked)
-        take_y(7, y_bank)
-        interleave_v(z_last[:, 0:P, :], z_rows[1][:, :, HALF:HALF + P])
-        quantize_y(7)
-        quantize_z(z_last, BANK + HALF, H)
+            out_1_first_half(i, drel_bank())
+        picked = pick_rows(GROUPS - 1)
+        dz_bank = transpose_dz(GROUPS - 1)
+        take_picked(last_piece, picked)
+        take_dz(GROUPS - 1, dz_bank)
+        interleave_vector(last_piece[:, 0:P, :], dz_slabs[1][:, :, PIECE:PIECE + P])
+        for i in range(F // P):
+            store(nc.scalar.copy, out_1_product(i, 1, drel_bank(), PIECE), out_1[i * P:(i + 1) * P, BANK:BANK + PIECE])
+        quantize_dz(GROUPS - 1)
+        quantize(dz_token_codes, E5M2, H - PIECE, flat(last_piece))
         for n in range(2):
-            store0(nc.scalar.copy, 3, n, out0_mx(3, n, score_bank()))
-        for i in range(8):
-            store0x(copies[(i + 1) % 2], i, out1_mx(i, H, score_bank() if i % 3 else spare_bank()))
+            store_out_0(nc.vector.tensor_copy, B - 1, n, out_0_product(B - 1, n, spare_bank()))
+        for i in range(F // P):
+            store(nc.scalar.copy if i % 2 else nc.vector.tensor_copy, out_1_product(i, 1, drel_bank()), out_1[i * P:(i + 1) * P, H - PIECE:H])

@@ -30,7 +30,7 @@ LAST_ROWS = P - T // PACK
 
 AHEAD = 3
 LOAD_AHEAD = 3
-PLAIN_S = (0, 8)
+PLAIN_S = ()
 CLOSING = UNITS - 5
 
 GPSIMD_SQUARES = 256

import math
from contextlib import ExitStack

import concourse.mybir as mybir
from concourse.masks import make_identity

B, L, S, T, F, H = 4, 512, 16, 128, 1024, 1024
FLOPS = 2 * B * T * S * L * H + 2 * 2 * B * T * F * H
BYTES = 2 * (B * L * H + B * T * F + F * H + B * L * T * S) + 4 * (B * S * H + B * T * H + B * T * F + F * H)

F32 = mybir.dt.float32
BF16 = mybir.dt.bfloat16
U32 = mybir.dt.uint32
U8 = mybir.dt.uint8
E4M3 = mybir.dt.float8_e4m3fn_x4
E5M2 = mybir.dt.float8_e5m2_x4
ALU = mybir.AluOpType
ACT = mybir.ActivationFunctionType

P = 128
PACK = 4
BANK = 512
PIECE = BANK // 2
BANK_TOKENS = BANK // S
UNIT_BANKS = T // BANK_TOKENS
GROUP = BANK // P
GROUPS = B * H // BANK
UNITS = GROUP * GROUPS
LAST_ROWS = P - T // PACK

AHEAD = 3
LOAD_AHEAD = 3
PLAIN_S = ()
CLOSING = UNITS - 5

GPSIMD_SQUARES = 256
GPSIMD_SQUARES_LAST_B = 384
VECTOR_SQUARES_ONE_PIECE = 512
VECTOR_SQUARES = 384


def spread(total, steps):
    done = [math.ceil(total * n / steps) for n in range(steps + 1)]
    return [done[n + 1] - done[n] for n in range(steps)]


def plan_fills(piece_counts, last_b_from):
    waiting = [(GROUP * k - 6, "t", k) for k in range(2, GROUPS)]
    waiting = waiting + [(GROUP * k + 5, "dz", k) for k in range(GROUPS - 1)]
    waiting = waiting + [(0, "w", i) for i in range(F // P)]
    waiting = waiting + [(12 + n, "out_0", (0, n)) for n in range(2)]
    waiting = waiting + [(2 * GROUP * b + 10, "out_0", (b, n)) for b in range(1, B - 1) for n in range(2)]
    fills = []
    for step in range(UNITS - 1):
        room = 2 if piece_counts[step + 1] == 2 else (1 if step >= last_b_from else 0)
        taken = [item for item in waiting if item[0] <= step][:room]
        waiting = [item for item in waiting if item not in taken]
        fills.append([item[1:] for item in taken])
    return fills + [[], [], []]


def tile_dynamicattention4_pa_v_kernel(tc, q, src, trg, Ws, b_s, Wt, b_t, s_key, t_key, grad_out,
                                                    out_0, out_1):
    nc = tc.nc
    with ExitStack() as ctx:
        sb = ctx.enter_context(tc.tile_pool(name="sb", bufs=1))
        ps = ctx.enter_context(tc.psum_pool(name="ps", bufs=1))
        ctx.enter_context(tc.manual_schedule())

        def drel_bank():
            return ps.tile([P, BANK], F32, name="drel_bank", bufs=UNIT_BANKS)

        def spare_bank():
            return ps.tile([P, BANK], F32, name="spare_bank", bufs=2)

        def mx_pair(name, width, bufs=1):
            words = sb.tile([P, width], U32, name=name + "_words", bufs=bufs, align_bytes=64)
            scales = sb.tile([P, width], U8, name=name + "_scales", bufs=bufs, align_bytes=64)
            return words, scales

        def quantize(pair, fmt, lo, values):
            cols = slice(lo, lo + values.shape[1] // PACK)
            nc.vector.quantize_mx(out=pair[0][:, cols].bitcast(fmt), scales=pair[1][:, cols], in_=values)

        def matmul_mx(bank, still, still_lo, still_fmt, moving, moving_lo, moving_fmt, start=True, stop=True):
            m_cols, n_cols = slice(still_lo, still_lo + P), slice(moving_lo, moving_lo + BANK)
            nc.tensor.matmul_mx(out=bank[:], lhsT=still[0][:, m_cols].bitcast(still_fmt), lhsT_scale=still[1][:, m_cols],
                                rhs=moving[0][:, n_cols].bitcast(moving_fmt), rhs_scale=moving[1][:, n_cols],
                                start=start, stop=stop)

        raw, codes = {}, {}
        code_bufs = {"g": 2 * UNIT_BANKS, "q": 4, "trg": 2}

        def load_slab(slab):
            tensor, b, block = slab
            if tensor == "g":
                rows = grad_out[b].rearrange("(p j) t s -> p j (t s)", j=PACK)
            elif tensor == "q":
                rows = q[b].rearrange("(p j) h -> p j h", j=PACK)
            else:
                rows = trg.rearrange("b t f -> (b t) f").rearrange("(p j) f -> p j f", j=PACK)
            raw[slab] = sb.tile([P, PACK, BANK], BF16, name="raw", bufs=2 * LOAD_AHEAD)
            nc.sync.dma_start(out=raw[slab][:], in_=rows[:, :, block * BANK:(block + 1) * BANK])

        def piece_tile(n):
            return sb.tile([P, PIECE, PACK], BF16, name="piece%d" % n, bufs=1, align_bytes=64)

        def interleave_vector(grouped, rows):
            nc.vector.tensor_copy(out=grouped, in_=rows.rearrange("p j c -> p c j"))

        def interleave_gpsimd(grouped, rows):
            nc.gpsimd.tensor_scalar(out=grouped, in0=rows.rearrange("p j c -> p c j"), scalar1=1.0, scalar2=1.0,
                                    op0=ALU.mult, op1=ALU.mult)

        def flat(grouped):
            return grouped[:].rearrange("p c j -> p (c j)")

        def quantize_slab(slab, lo, grouped):
            if lo == 0:
                codes[slab] = mx_pair(slab[0], BANK, code_bufs[slab[0]])
            quantize(codes[slab], E5M2 if slab[0] == "g" else E4M3, lo, flat(grouped))

        first_slabs = [("q", 0, 0)] + [("g", 0, a) for a in range(UNIT_BANKS)]
        slabs = []
        for b in range(1, B):
            slabs = slabs + [("q", b - 1, 1)] + [("g", b, a) for a in range(UNIT_BANKS)] + [("q", b, 0)]
        slabs = slabs + [("q", B - 1, 1), ("trg", 0, 0), ("trg", 0, 1)]
        pieces = [(slab, lo) for slab in slabs for lo in (0, PIECE)]
        per_b = 2 * (UNIT_BANKS + 2)
        piece_counts = spread(per_b, 2 * GROUP - 1) + spread(per_b, 2 * GROUP) * (B - 2)
        last_b_from = len(piece_counts)
        piece_counts = piece_counts + spread(len(pieces) - sum(piece_counts), CLOSING + 1 - last_b_from)
        piece_counts = piece_counts + [0] * (UNITS - len(piece_counts))
        piece_starts = [sum(piece_counts[:n]) for n in range(UNITS + 1)]
        fills = plan_fills(piece_counts, last_b_from)

        t_rows, t_cols = {}, {}

        def load_t(k):
            b, half = divmod(k, 2)
            t_rows[k] = sb.tile([P, BANK], F32, name="t_rows", bufs=2)
            nc.sync.dma_start(out=t_rows[k][:], in_=t_key[b][:, half * BANK:(half + 1) * BANK])

        def transpose_blocks(rows):
            bank = spare_bank()
            for c in range(GROUP):
                nc.tensor.transpose(bank[:, c * P:(c + 1) * P], rows[:, c * P:(c + 1) * P], ident[:])
            return bank

        def take_t(k, bank):
            t_cols[k] = sb.tile([P, BANK], F32, name="t_cols", bufs=3)
            nc.vector.tensor_copy(out=t_cols[k][:], in_=bank[:])

        rel, drel, weighted, dz_sum, dz_rows = {}, {}, {}, {}, {}

        def tanh(u, s_lo, s_hi):
            k, c = divmod(u, GROUP)
            b, half = divmod(k, 2)
            if s_lo == 0:
                rel[u] = sb.tile([P, S, T], F32, name="rel", bufs=AHEAD + 1)
            for s in range(s_lo, s_hi):
                col = c * P + 2 * (b * S + s) + half
                nc.scalar.activation(out=rel[u][:, s, :], in_=t_cols[k][:, c * P:(c + 1) * P], func=ACT.Tanh,
                                     bias=s_cols[:, col:col + 1])

        def square_shares(u):
            step = u - 1
            on_gpsimd, on_vector = 0, 0
            if step >= 1:
                one_piece = piece_counts[step] < 2
                on_vector = VECTOR_SQUARES_ONE_PIECE if one_piece and step < last_b_from else VECTOR_SQUARES
                if one_piece and step < UNITS - 2:
                    on_gpsimd = GPSIMD_SQUARES if step < last_b_from else GPSIMD_SQUARES_LAST_B
            return S * T - on_gpsimd - on_vector, S * T - on_gpsimd

        def rel_columns(u, lo, hi):
            return rel[u][:].rearrange("p s t -> p (s t)")[:, lo:hi]

        def square_scalar(u):
            part = rel_columns(u, 0, square_shares(u)[0])
            nc.scalar.activation(out=part, in_=part, func=ACT.Square, bias=zero[:])

        def square(engine, u, lo, hi):
            if hi > lo:
                part = rel_columns(u, lo, hi)
                engine.tensor_tensor(out=part, in0=part, in1=part, op=ALU.mult)

        def scalar_step(u):
            if u < UNITS:
                tanh(u, 0, 2)
            if u - 1 < UNITS:
                square_scalar(u - 1)
            if u < UNITS:
                tanh(u, 2, S)

        def drel_product(u, a):
            k, c = divmod(u, GROUP)
            b, half = divmod(k, 2)
            drel[u, a] = drel_bank()
            matmul_mx(drel[u, a], codes["q", b, half], c * P, E4M3, codes["g", b, a], 0, E5M2)

        def weigh(u, a):
            if a == 0:
                weighted[u] = sb.tile([P, S, T], F32, name="weighted", bufs=3)
            tokens = slice(a * BANK_TOKENS, (a + 1) * BANK_TOKENS)
            nc.vector.scalar_tensor_tensor(out=weighted[u][:, :, tokens], in0=rel[u][:, :, tokens], scalar=1.0,
                                           in1=drel[u, a][:].rearrange("p (t s) -> p s t", s=S),
                                           op0=ALU.subtract, op1=ALU.mult)

        def sum_over_s(u, s_lo, s_hi):
            if s_lo == 0:
                dz_sum[u] = ps.tile([P, P], F32, name="dz_sum", bufs=2)
            for s in range(s_lo, s_hi):
                nc.tensor.matmul(out=dz_sum[u][:], lhsT=weighted[u][:, s, :], rhs=ident[:],
                                 is_transpose=(s not in PLAIN_S or u >= UNITS - 3), start=(s == 0), stop=(s == S - 1))

        def round_dz(u):
            k, c = divmod(u, GROUP)
            if c == 0:
                dz_rows[k] = sb.tile([P, BANK], BF16, name="dz_rows", bufs=3)
            nc.vector.tensor_scalar(out=dz_rows[k][:, c * P:(c + 1) * P], in0=dz_sum[u][:],
                                    scalar1=-1.0 / math.sqrt(H), scalar2=None, op0=ALU.mult)

        def regroup(k, lo, hi):
            b, half = divmod(k, 2)
            rows = slice(b * T // PACK, (b + 1) * T // PACK)
            for j in range(PACK):
                nc.sync.dma_start(out=dz_slabs[half][rows, j, lo:hi], in_=dz_rows[k][j::PACK, lo:hi])

        def round_and_regroup(u):
            k, c = divmod(u, GROUP)
            round_dz(u)
            if k < GROUPS - 2 and c == GROUP - 1:
                regroup(k, 0, BANK)
            if k >= GROUPS - 2 and c == 1:
                regroup(k, 0, PIECE)
            if k >= GROUPS - 2 and c == 2:
                regroup(k, PIECE, PIECE + P)

        def pick_rows(k):
            bank = spare_bank()
            for j in range(PACK):
                nc.tensor.matmul(out=bank[:, j * P:(j + 1) * P], lhsT=pick[:, j, :], rhs=dz_rows[k][:, BANK - P:BANK],
                                 start=True, stop=True)
            return bank

        def take_picked(grouped, bank):
            nc.vector.tensor_copy(out=grouped[LAST_ROWS:P, P:PIECE, :],
                                  in_=bank[LAST_ROWS:P, :].rearrange("p (j c) -> p c j", j=PACK))

        def transpose_words(bank, block, words):
            for e in range(2):
                cols = slice((2 * block + e) * P, (2 * block + e + 1) * P)
                nc.tensor.transpose(bank[:, cols], words[:, e::2], ident[:])

        w_rows, dz_pairs, dz_codes = {}, {}, {}

        def load_w(i):
            w_rows[i] = sb.tile([P, H], BF16, name="w_rows", bufs=4)
            nc.sync.dma_start(out=w_rows[i][:], in_=Wt[i * P:(i + 1) * P, :])

        def transpose_w(i):
            bank = spare_bank()
            for g in range(2):
                transpose_words(bank, g, w_rows[i][:, g * BANK:(g + 1) * BANK].bitcast(F32))
            return bank

        def take_w(i, bank):
            pairs = w_pairs[:].rearrange("p (g f e) -> p g f e", g=2, e=2)
            nc.vector.tensor_copy(out=pairs[:, :, i * P:(i + 1) * P, :],
                                  in_=bank[:].rearrange("p (g e f) -> p g f e", g=2, e=2))

        def quantize_w(g, n):
            lo = g * F + n * BANK
            quantize(w_codes, E4M3, lo, w_pairs[:, 2 * lo:2 * (lo + BANK)].bitcast(BF16))

        def transpose_dz(k):
            bank = spare_bank()
            transpose_words(bank, 0, dz_rows[k][:].bitcast(F32))
            return bank

        def take_dz(k, bank):
            dz_pairs[k] = sb.tile([P, 2 * T], F32, name="dz_pairs", bufs=2, align_bytes=64)
            nc.vector.tensor_copy(out=dz_pairs[k][:].rearrange("p (t e) -> p t e", e=2),
                                  in_=bank[:, 0:2 * T].rearrange("p (e t) -> p t e", e=2))

        def quantize_dz(k):
            dz_codes[k] = mx_pair("dz_features", T, GROUPS)
            quantize(dz_codes[k], E5M2, 0, dz_pairs[k][:].bitcast(BF16))

        def out_0_product(b, n, bank):
            for g in range(2):
                matmul_mx(bank, dz_codes[2 * b + g], 0, E5M2, w_codes, g * F + n * BANK, E4M3, g == 0, g == 1)
            return bank

        def out_1_product(i, half, bank, back=0):
            block, c = divmod(i, GROUP)
            matmul_mx(bank, codes["trg", 0, block], c * P, E4M3, dz_token_codes, half * BANK - back, E5M2)
            return bank

        def store(copy, bank, rows):
            width = rows.shape[1]
            result = sb.tile([P, width], F32, name="result", bufs=10)
            copy(out=result[:], in_=bank[:, BANK - width:BANK])
            nc.sync.dma_start(out=rows, in_=result[:])

        def store_out_0(copy, b, n, bank):
            store(copy, bank, out_0[b][:, n * BANK:(n + 1) * BANK])

        result_pairs = {}

        def out_1_first_half(i, bank):
            pair, n = divmod(i, 2)
            out_1_product(i, 0, bank)
            if n == 0:
                result_pairs[pair] = sb.tile([P, 2, BANK], F32, name="result_pair", bufs=3)
            nc.scalar.copy(out=result_pairs[pair][:, n, :], in_=bank[:])
            if n == 1:
                rows = out_1[2 * pair * P:2 * (pair + 1) * P, 0:BANK].rearrange("(n p) h -> p n h", p=P)
                nc.scalar.dma_start(out=rows, in_=result_pairs[pair][:])

        load_t(0)
        s_rows = sb.tile([P, BANK], F32, name="s_rows")
        nc.sync.dma_start(out=s_rows[:], in_=s_key.rearrange("b s (half h) -> (b s half) h", half=2))
        for slab in first_slabs + slabs[:1]:
            load_slab(slab)
        load_t(1)

        ident = sb.tile([P, P], F32, name="ident")
        make_identity(nc, ident[:])
        seed = sb.tile([P, 1], F32, name="seed")
        nc.vector.memset(seed[:], 0.0)
        zero = sb.tile([P, 1], F32, name="zero")
        nc.scalar.activation(out=zero[:], in_=seed[:], func=ACT.Tanh, bias=seed[:])
        pick = sb.tile([P, PACK, P], BF16, name="pick")
        nc.gpsimd.memset(pick[:], 0.0)
        nc.gpsimd.tensor_copy(out=pick[:, :, LAST_ROWS:P], in_=ident[:].rearrange("p (i j) -> p j i", j=PACK))

        w_pairs = sb.tile([P, 2 * F * 2], F32, name="w_pairs", align_bytes=64)
        w_codes = mx_pair("w", 2 * F)
        dz_token_codes = mx_pair("dz_tokens", H)
        dz_slabs = [sb.tile([P, PACK, BANK], BF16, name="dz_slab%d" % half) for half in range(2)]

        t_bank = transpose_blocks(t_rows[0])
        s_bank = transpose_blocks(s_rows)
        take_t(0, t_bank)
        s_cols = sb.tile([P, BANK], F32, name="s_cols")
        nc.vector.tensor_copy(out=s_cols[:], in_=s_bank[:])

        waiting = None
        for slab in first_slabs[:-1]:
            grouped = sb.tile([P, BANK, PACK], BF16, name="first_grouped", bufs=2, align_bytes=64)
            interleave_vector(grouped[:], raw[slab][:])
            if waiting is not None:
                quantize_slab(*waiting)
            waiting = (slab, 0, grouped)
        slab = first_slabs[-1]
        halves = [(slab, n * PIECE, piece_tile(n)) for n in range(2)]
        for slab, lo, grouped in halves:
            interleave_vector(grouped[:], raw[slab][:, :, lo:lo + PIECE])
        for item in [waiting] + halves:
            quantize_slab(*item)

        loaded = LOAD_AHEAD
        for slab in slabs[1:loaded]:
            load_slab(slab)
        for kind, i in fills[0] + fills[1]:
            load_w(i)
        for a in range(UNIT_BANKS):
            drel_product(0, a)
        filled = [("t", 1, transpose_blocks(t_rows[1]))]
        tanh(0, 0, S)
        for u in range(1, AHEAD):
            scalar_step(u)

        one_piece_steps = [step for step in range(last_b_from) if piece_counts[step] == 1]
        w_done = [1 + max(step for step in range(UNITS) for kind, i in fills[step] if kind == "w" and i // GROUP == n)
                  for n in range(2)]
        w_steps = {}
        for n in range(2):
            for g, step in enumerate([step for step in one_piece_steps if step > w_done[n]][:2]):
                w_steps[step] = (g, n)

        for step in range(UNITS):
            last = step == UNITS - 1
            while loaded < len(slabs) and 2 * loaded < piece_starts[min(step + LOAD_AHEAD + 1, UNITS)]:
                load_slab(slabs[loaded])
                loaded = loaded + 1
            for kind, i in fills[step + 2]:
                if kind == "w":
                    load_w(i)
                if kind == "t":
                    load_t(i)

            grouped_pieces = []
            for n, (slab, lo) in enumerate(pieces[piece_starts[step]:piece_starts[step + 1]]):
                grouped = piece_tile(n)
                interleave_gpsimd(grouped[:], raw[slab][:, :, lo:lo + PIECE])
                grouped_pieces.append((slab, lo, grouped))
            dz_piece = None
            if step == CLOSING + 1 or last:
                half = int(last)
                dz_piece = (half * BANK, piece_tile(0))
                interleave_gpsimd(dz_piece[1][:], dz_slabs[half][:, :, 0:PIECE])
            if step == CLOSING + 2:
                dz_piece = (PIECE, piece_tile(0))
                interleave_gpsimd(dz_piece[1][0:LAST_ROWS, P:PIECE, :], dz_slabs[0][0:LAST_ROWS, :, BANK - P:BANK])
                interleave_gpsimd(dz_piece[1][:, 0:P, :], dz_slabs[0][:, :, PIECE:PIECE + P])
                filled.append(("picked", dz_piece[1], pick_rows(GROUPS - 2)))
            if not last:
                square(nc.gpsimd, step + 1, square_shares(step + 1)[1], S * T)

            scalar_step(step + AHEAD)

            for a in (0, 1):
                weigh(step, a)
                if last:
                    out_1_first_half(4 + a, drel_bank())
                else:
                    drel_product(step + 1, a)
            if step > 0:
                sum_over_s(step - 1, S // 2, S)
            if 2 <= step <= CLOSING:
                round_and_regroup(step - 2)
            if step == UNITS - 2:
                for i in (0, 1):
                    out_1_first_half(i, spare_bank())
            for a in (2, 3):
                weigh(step, a)
                if not last:
                    drel_product(step + 1, a)
            dz_taken = []
            for kind, i, bank in filled:
                if kind == "t":
                    take_t(i, bank)
                if kind == "w":
                    take_w(i, bank)
                if kind == "dz":
                    take_dz(i, bank)
                    dz_taken.append(i)
                if kind == "picked":
                    take_picked(i, bank)
                if kind == "out_0":
                    store_out_0(nc.vector.tensor_copy, *i, bank)
            sum_over_s(step, 0, S if last else S // 2)
            if step == UNITS - 2:
                for i in (2, 3):
                    out_1_first_half(i, spare_bank())

            if not last:
                square(nc.vector, step + 1, *square_shares(step + 1))
            for k in dz_taken:
                quantize_dz(k)
            if step in w_steps:
                quantize_w(*w_steps[step])
            for item in grouped_pieces:
                quantize_slab(*item)
            if last:
                round_and_regroup(step - 1)
                last_piece = piece_tile(1)
                interleave_vector(last_piece[0:LAST_ROWS, P:PIECE, :], dz_slabs[1][0:LAST_ROWS, :, BANK - P:BANK])
                round_dz(step)
            if dz_piece is not None:
                quantize(dz_token_codes, E5M2, dz_piece[0], flat(dz_piece[1]))
            if CLOSING <= step < UNITS - 1:
                round_and_regroup(step - 1)

            filled = []
            for kind, i in fills[step]:
                if kind == "t":
                    filled.append((kind, i, transpose_blocks(t_rows[i])))
                if kind == "w":
                    filled.append((kind, i, transpose_w(i)))
                if kind == "dz":
                    filled.append((kind, i, transpose_dz(i)))
                if kind == "out_0":
                    filled.append((kind, i, out_0_product(*i, spare_bank())))

        for i in (6, 7):
            out_1_first_half(i, drel_bank())
        picked = pick_rows(GROUPS - 1)
        dz_bank = transpose_dz(GROUPS - 1)
        take_picked(last_piece, picked)
        take_dz(GROUPS - 1, dz_bank)
        interleave_vector(last_piece[:, 0:P, :], dz_slabs[1][:, :, PIECE:PIECE + P])
        for i in range(F // P):
            store(nc.scalar.copy, out_1_product(i, 1, drel_bank(), PIECE), out_1[i * P:(i + 1) * P, BANK:BANK + PIECE])
        quantize_dz(GROUPS - 1)
        quantize(dz_token_codes, E5M2, H - PIECE, flat(last_piece))
        for n in range(2):
            store_out_0(nc.vector.tensor_copy, B - 1, n, out_0_product(B - 1, n, spare_bank()))
        for i in range(F // P):
            store(nc.scalar.copy if i % 2 else nc.vector.tensor_copy, out_1_product(i, 1, drel_bank()), out_1[i * P:(i + 1) * P, H - PIECE:H])
